import numpy as np
import ml_dtypes


def mxq(x, axis, fmt="e4m3"):
    dtype, down = {"e4m3": (ml_dtypes.float8_e4m3fn, 7), "e5m2": (ml_dtypes.float8_e5m2, 14)}[fmt]
    v = np.moveaxis(np.asarray(x, np.float32).astype(ml_dtypes.bfloat16).astype(np.float64), axis, -1)
    blocks = v.reshape(v.shape[:-1] + (-1, 32))
    amax = np.abs(blocks).max(-1, keepdims=True)
    byte = np.maximum(np.where(amax > 0, np.frexp(amax)[1] - 1 + 127, 0) - down, 1)
    scale = np.exp2(byte - 127.0)
    codes = (blocks / scale).astype(np.float32).astype(dtype).astype(np.float64)
    return np.moveaxis((codes * scale).reshape(v.shape), -1, axis)


WIDE = False


def mx_kscale(k):
    if not WIDE:
        return np.ones(k)
    levels = np.array([10, -10, 5, -5, 0])
    if k % 512:
        return np.exp2(np.random.permutation(np.resize(levels, k // 32))).repeat(32)
    a = np.empty((k // 512, 16))
    for p in range(k // 512):
        a[p, :8] = np.random.permutation(np.resize(levels, 8))
        for g in range(8):
            far = levels[np.abs(levels - a[p, g]) >= 10]
            a[p, g + 8] = far[np.random.randint(len(far))]
    return np.exp2(a.ravel()).repeat(32)


BF16 = ml_dtypes.bfloat16


def bf(x):
    return np.asarray(x, np.float32).astype(BF16)


def f64(x):
    return np.asarray(x).astype(np.float64)


B, L, D, T = 1024, 16, 512, 8
F = 2 * D
LN_EPS = 1e-5


def erf(v):
    a = np.minimum(np.abs(v), 6.0)
    term = a.copy()
    total = a.copy()
    for n in range(1, 200):
        term = term * (2.0 * a * a / (2 * n + 1))
        total = total + term
    return np.sign(v) * (2.0 / np.sqrt(np.pi)) * np.exp(-a * a) * total


def gelu_erf(v):
    return 0.5 * v * (1.0 + erf(v / np.sqrt(2.0)))


def draw0():
    s, t = mx_kscale(D), mx_kscale(F)
    counts = np.random.randint(1, T + 1, B)
    counts[0] = T
    target_mask = (np.arange(L)[None, :] < counts[:, None]).astype(np.float64)
    context_mask = 1.0 - target_mask
    context_mask[np.random.random(B) < 0.125] = 0.0
    return {"context_repr": bf(np.random.standard_normal((B, L, D)) * (0.75 * np.sqrt(L)) * s),
            "target_mask": bf(target_mask),
            "context_mask": bf(context_mask),
            "W1": bf(np.random.standard_normal((D, F)) / np.sqrt(D) / s[:, None]),
            "b1": bf(np.random.standard_normal(F) * 0.5),
            "gamma": bf((1.0 + 0.1 * np.random.standard_normal(F)) * t),
            "beta": bf(0.2 * np.random.standard_normal(F) * t),
            "W2": bf(np.random.standard_normal((F, D)) / np.sqrt(F) / t[:, None]),
            "b2": bf(np.random.standard_normal(D) * 0.3),
            "num_targets": T}


def core(context_repr, target_mask, context_mask, W1, b1, gamma, beta, W2, b2, num_targets):
    ctx_count = f64(context_mask).sum(axis=-1)
    ctx_sum = f64(context_repr).sum(axis=1)
    mean = ctx_sum / np.maximum(ctx_count, 1.0)[:, None]
    mean = np.where((ctx_count > 0)[:, None], mean, 0.0)
    h = gelu_erf((mxq(mean, 1, "e4m3") @ mxq(f64(W1), 0, "e4m3")) + f64(b1))
    mu = h.mean(axis=-1, keepdims=True)
    var = ((h - mu) ** 2).mean(axis=-1, keepdims=True)
    hn = (h - mu) / np.sqrt(var + LN_EPS) * f64(gamma) + f64(beta)
    out = (mxq(hn, 1, "e4m3") @ mxq(f64(W2), 0, "e4m3")) + f64(b2)
    tgt_counts = f64(target_mask).sum(axis=-1)
    valid = np.arange(num_targets)[None, :] < tgt_counts[:, None]
    return np.where(valid[:, :, None], out[:, None, :], 0.0)


def e4m3fn_bytes(y):
    return np.clip(np.asarray(y, np.float64), -448.0, 448.0).astype(np.float32).astype(ml_dtypes.float8_e4m3fn).view(np.uint8)


def e4m3fn_values(b):
    return np.asarray(b, np.uint8).view(ml_dtypes.float8_e4m3fn).astype(np.float64)


def setup_inputs():
    d = draw0()
    x0 = np.asarray(d['W2']).astype(np.float64)
    s = (np.max(np.abs(x0), axis=(1,), keepdims=True) / 448.0).astype(np.float32)
    out = {}
    for k, v in d.items():
        if k == 'W2':
            out['W2_bytes'] = e4m3fn_bytes(x0 / s.astype(np.float64))
            out['W2_scale'] = s
        else:
            out[k] = v
    return out


def reference(context_repr, target_mask, context_mask, W1, b1, gamma, beta, W2_bytes, W2_scale, b2, num_targets):
    return core(context_repr, target_mask, context_mask, W1, b1, gamma, beta, e4m3fn_values(W2_bytes) * W2_scale.astype(np.float64), b2, num_targets)

@@ -1,0 +1,363 @@
+from contextlib import ExitStack
+
+import concourse.mybir as mybir
+from concourse.masks import make_identity
+
+B, L, D, T = 1024, 16, 512, 8
+F = 2 * D
+LN_EPS = 1e-5
+
+FLOPS = 2 * B * D * F * 2
+P = 128
+NT = B // P
+HC = 8
+
+F32 = mybir.dt.float32
+BF16 = mybir.dt.bfloat16
+U32 = mybir.dt.uint32
+U8 = mybir.dt.uint8
+FP8 = mybir.dt.float8_e4m3fn
+FP8X4 = mybir.dt.float8_e4m3fn_x4
+ALU = mybir.AluOpType
+ACT = mybir.ActivationFunctionType
+X = mybir.AxisListType.X
+
+
+def tile_simplepredictor_t_kernel(
+    tc, context_repr, target_mask, context_mask, W1, b1, gamma, beta, W2_bytes, W2_scale, b2, num_targets, out
+):
+    nc = tc.nc
+    with ExitStack() as es:
+        keep = es.enter_context(tc.tile_pool(name="keep", bufs=1))
+        ctxp = es.enter_context(tc.tile_pool(name="ctxp", bufs=8))
+        work = es.enter_context(tc.tile_pool(name="work", bufs=2))
+        outp = es.enter_context(tc.tile_pool(name="outp", bufs=8))
+        psum = es.enter_context(tc.psum_pool(name="psum", bufs=2))
+
+        es.enter_context(tc.manual_schedule())
+
+        cmask = keep.tile([P, 8, L], BF16)
+        nc.scalar.dma_start(out=cmask[:], in_=context_mask.rearrange("(p i) l -> p i l", i=8))
+        tmask = keep.tile([P, 8, L], BF16)
+        nc.scalar.dma_start(out=tmask[:], in_=target_mask.rearrange("(p i) l -> p i l", i=8))
+        b1c = keep.tile([P, 8], BF16)
+        nc.scalar.dma_start(out=b1c[:], in_=b1.rearrange("(p i) -> p i", i=8))
+        gac = keep.tile([P, 8], BF16)
+        nc.scalar.dma_start(out=gac[:], in_=gamma.rearrange("(p i) -> p i", i=8))
+        bec = keep.tile([P, 8], BF16)
+        nc.scalar.dma_start(out=bec[:], in_=beta.rearrange("(p i) -> p i", i=8))
+        b2c = keep.tile([P, 4], BF16)
+        nc.scalar.dma_start(out=b2c[:], in_=b2.rearrange("(p i) -> p i", i=4))
+        w2s = keep.tile([P, 2, 4], F32)
+        nc.scalar.dma_start(out=w2s[:], in_=W2_scale.rearrange("(g p j) o -> p g (j o)", g=2, j=4))
+
+        w1view = W1.rearrange("(p j) c -> p j c", j=4)
+        w1raw = []
+        for n in range(2):
+            raw = keep.tile([P, 4, 512], BF16, name="w1raw%d" % n)
+            nc.sync.dma_start(out=raw[:], in_=w1view[:, :, 512 * n : 512 * n + 512])
+            w1raw.append(raw)
+
+        ctx_rows = context_repr.rearrange("b l d -> (b l) d").rearrange("(c p) d -> p c d", p=P)
+        ctx_tiles = {}
+
+        def load_ctx(i):
+            for half in range(2):
+                t = ctxp.tile([P, HC, D], BF16, tag="ctx", name="ctx")
+                c0 = 16 * i + HC * half
+                nc.sync.dma_start(out=t[:], in_=ctx_rows[:, c0 : c0 + HC, :])
+                ctx_tiles[(i, half)] = t
+
+        load_ctx(0)
+        w2b = keep.tile([P, 2, 4, 512], U8)
+        nc.sync.dma_start(
+            out=w2b[:].rearrange("p g j n -> p g (j n)"), in_=W2_bytes.rearrange("(g p j) n -> p g (j n)", g=2, j=4)
+        )
+        for i in range(1, 4):
+            load_ctx(i)
+
+        identf = keep.tile([P, P], F32)
+        make_identity(nc, identf[:])
+        neghalf = keep.tile([P, 1], F32)
+        nc.gpsimd.memset(neghalf[:], -0.5)
+        jidx = keep.tile([P, T], F32)
+        nc.gpsimd.iota(jidx[:], pattern=[[1, T]], base=0, channel_multiplier=0, allow_small_or_imprecise_dtypes=True)
+        warm = keep.tile([P, 1], F32)
+        nc.gpsimd.memset(warm[:], 0.0)
+        warm2 = keep.tile([P, 1], F32)
+        nc.scalar.activation(out=warm2[:], in_=warm[:], func=ACT.Gelu)
+
+        identb = keep.tile([P, P], BF16)
+        nc.vector.tensor_copy(out=identb[:], in_=identf[:])
+        self_f = keep.tile([P, 8], F32)
+        sel = keep.tile([P, 8], BF16)
+        nc.vector.tensor_reduce(out=self_f[:], in_=identf[:].rearrange("p (g q) -> p g q", q=16), axis=X, op=ALU.add)
+        nc.vector.tensor_copy(out=sel[:], in_=self_f[:])
+        modq = keep.tile([P, 16], F32)
+        nc.vector.tensor_reduce(out=modq[:], in_=identf[:].rearrange("p (g q) -> p q g", q=16), axis=X, op=ALU.add)
+
+        cnt = keep.tile([P, 8], F32)
+        nc.vector.tensor_reduce(out=cnt[:], in_=cmask[:], axis=X, op=ALU.add)
+        cmax = keep.tile([P, 8], F32)
+        nc.vector.tensor_scalar_max(cmax[:], cnt[:], 1.0)
+        crec = keep.tile([P, 8], F32)
+        nc.vector.reciprocal(crec[:], cmax[:])
+        rcp = keep.tile([P, 8], F32)
+        nc.vector.scalar_tensor_tensor(out=rcp[:], in0=cnt[:], scalar=0.0, in1=crec[:], op0=ALU.is_gt, op1=ALU.mult)
+
+        n8 = keep.tile([P, 8], F32)
+        nc.vector.tensor_reduce(out=n8[:], in_=tmask[:], axis=X, op=ALU.add)
+        nl = keep.tile([P, 16, 8], BF16)
+        nc.vector.tensor_tensor(
+            out=nl[:],
+            in0=n8[:].unsqueeze(1).to_broadcast([P, 16, 8]),
+            in1=modq[:].unsqueeze(2).to_broadcast([P, 16, 8]),
+            op=ALU.mult,
+        )
+
+        rcpb = keep.tile([P, B], F32)
+        for k in range(2):
+            pr = psum.tile([P, 4, P], F32, tag="h", bufs=4, name="pr")
+            for i in range(4):
+                col = rcp[:, 4 * k + i : 4 * k + i + 1]
+                nc.tensor.transpose(pr[:, i, :], col.to_broadcast([P, P]), identf[:])
+            nc.scalar.copy(
+                out=rcpb[:].rearrange("p (n i) -> p n i", i=8)[:, :, 4 * k : 4 * k + 4],
+                in_=pr[:].rearrange("p i n -> p n i"),
+            )
+
+        def spread(col, width, name):
+            per = width // P
+            dst = keep.tile([P, width], BF16, name=name)
+            pv = psum.tile([P, per, P], BF16, tag="h", bufs=4, name="pv")
+            for i in range(per):
+                nc.tensor.transpose(pv[:, i, :], col[:, i : i + 1].to_broadcast([P, P]), identb[:])
+            nc.scalar.copy(out=dst[:].rearrange("p (n i) -> p n i", i=per), in_=pv[:].rearrange("p i n -> p n i"))
+            return dst
+
+        b1b = spread(b1c, F, "b1b")
+
+        w1c = keep.tile([P, F], U32, align_bytes=64)
+        w1s = keep.tile([P, F], U8, align_bytes=64)
+        w1g = []
+        for n in range(2):
+            g = keep.tile([P, 512, 4], BF16, align_bytes=64, name="w1g%d" % n)
+            eng_copy = nc.vector.tensor_copy if n == 0 else nc.scalar.copy
+            eng_copy(out=g[:], in_=w1raw[n][:].rearrange("p j c -> p c j"))
+            w1g.append(g)
+
+        def quant_w1(n):
+            cols = slice(512 * n, 512 * n + 512)
+            nc.vector.quantize_mx(
+                out=w1c[:, cols].bitcast(FP8X4), scales=w1s[:, cols], in_=w1g[n][:].rearrange("p c j -> p (c j)")
+            )
+
+        w2w = keep.tile([P, 2, 4, 512], BF16)
+        w2g = [keep.tile([P, 512, 4], BF16, align_bytes=64, name="w2g%d" % g) for g in range(2)]
+        w2c = keep.tile([P, 2, 512], U32, align_bytes=64)
+        w2sc = keep.tile([P, 2, 512], U8, align_bytes=64)
+
+        def widen_w2(g):
+            for j in range(4):
+                nc.scalar.activation(
+                    out=w2w[:, g, j, :], in_=w2b[:, g, j, :].bitcast(FP8), func=ACT.Copy, scale=w2s[:, g, j : j + 1]
+                )
+
+        def inter_w2(g):
+            nc.vector.tensor_copy(out=w2g[g][:], in_=w2w[:, g].rearrange("p j n -> p n j"))
+
+        def quant_w2(g):
+            nc.vector.quantize_mx(
+                out=w2c[:, g, :].bitcast(FP8X4), scales=w2sc[:, g, :], in_=w2g[g][:].rearrange("p n j -> p (n j)")
+            )
+
+        st = {}
+
+        def pool(i, part):
+            if part == 0:
+                st["ps", i] = psum.tile([P, 4, P], F32, tag="pool", name="ps")
+            ps = st["ps", i]
+            for c in range(4 * part, 4 * part + 4):
+                x = ctx_tiles[(i, c // HC)]
+                for t in range(4):
+                    nc.tensor.matmul(
+                        out=ps[:, t, 8 * c : 8 * c + 8], lhsT=x[:, c % HC, t:D:4], rhs=sel[:], start=True, stop=True
+                    )
+
+        def scale_mean(i):
+            m = work.tile([P, P, 4], BF16, align_bytes=64, tag="mean", name="mean")
+            nc.vector.tensor_tensor(
+                out=m[:],
+                in0=st["ps", i][:].rearrange("p t b -> p b t"),
+                in1=rcpb[:, P * i : P * i + P].unsqueeze(2).to_broadcast([P, P, 4]),
+                op=ALU.mult,
+            )
+            st["mean", i] = m
+
+        def quant_mean(i):
+            c = work.tile([P, P], U32, align_bytes=64, tag="mc", name="mc")
+            s = work.tile([P, P], U8, align_bytes=64, tag="ms", name="ms")
+            nc.vector.quantize_mx(
+                out=c[:].bitcast(FP8X4), scales=s[:], in_=st["mean", i][:].rearrange("p b t -> p (b t)")
+            )
+            st["mc", i], st["ms", i] = c, s
+
+        def mm1(i):
+            st["ph", i] = []
+            for n in range(2):
+                ph = psum.tile([P, 512], F32, tag="h", bufs=4, name="ph")
+                cols = slice(512 * n, 512 * n + 512)
+                nc.tensor.matmul_mx(
+                    out=ph[:],
+                    lhsT=st["mc", i][:].bitcast(FP8X4),
+                    lhsT_scale=st["ms", i][:],
+                    rhs=w1c[:, cols].bitcast(FP8X4),
+                    rhs_scale=w1s[:, cols],
+                    start=True,
+                    stop=True,
+                )
+                st["ph", i].append(ph)
+
+        def bias_gelu(i):
+            v = work.tile([P, F], F32, tag="v", name="v")
+            h = work.tile([P, F], F32, tag="h", name="h")
+            for n in range(2):
+                cols = slice(512 * n, 512 * n + 512)
+                nc.vector.tensor_tensor(out=v[:, cols], in0=st["ph", i][n][:], in1=b1b[:, cols], op=ALU.add)
+                nc.scalar.activation(out=h[:, cols], in_=v[:, cols], func=ACT.Gelu)
+            st["h", i] = h
+
+        def stats(i):
+            bs = work.tile([P, 2, 6], F32, tag="bs", name="bs")
+            for n in range(2):
+                nc.vector.bn_stats(out=bs[:, n, :], in_=st["h", i][:, 512 * n : 512 * n + 512])
+            mv = work.tile([P, 2], F32, tag="mv", name="mv")
+            nc.vector.bn_aggr(out=mv[:], in_=bs[:].rearrange("p n s -> p (n s)"))
+            ve = work.tile([P, 1], F32, tag="ve", name="ve")
+            nc.gpsimd.tensor_scalar_add(ve[:], mv[:, 1:2], LN_EPS)
+            rs = work.tile([P, 1], F32, tag="rs", name="rs")
+            nc.gpsimd.tensor_tensor(out=rs[:], in0=ve[:], in1=neghalf[:], op=ALU.pow)
+            st["mv", i], st["rs", i] = mv, rs
+
+        def norm(i):
+            t1 = work.tile([P, F], F32, tag="t1", name="t1")
+            nc.vector.scalar_tensor_tensor(
+                out=t1[:], in0=st["h", i][:], scalar=st["mv", i][:, 0:1], in1=gab[:], op0=ALU.subtract, op1=ALU.mult
+            )
+            hn = work.tile([P, F], BF16, tag="hn", name="hn")
+            nc.vector.scalar_tensor_tensor(
+                out=hn[:], in0=t1[:], scalar=st["rs", i][:], in1=beb[:], op0=ALU.mult, op1=ALU.add
+            )
+            st["hn", i] = hn
+
+        def turn(i):
+            xt = psum.tile([P, 4, P], F32, tag="xt", bufs=1, name="xt")
+            words = st["hn", i][:].bitcast(F32)
+            for g in range(2):
+                for u in range(2):
+                    nc.tensor.transpose(xt[:, 2 * g + u, :], words[:, 256 * g + u : 256 * g + 256 : 2], identf[:])
+            hg = work.tile([P, 2 * P * 4], BF16, align_bytes=64, tag="hg", name="hg")
+            nc.scalar.copy(
+                out=hg[:].bitcast(F32).rearrange("p (g r u) -> p g r u", g=2, u=2),
+                in_=xt[:].rearrange("p (g u) r -> p g r u", g=2),
+            )
+            st["hg", i] = hg
+
+        def quant_hn(i):
+            c = work.tile([P, 2 * P], U32, align_bytes=64, tag="hc", name="hc")
+            s = work.tile([P, 2 * P], U8, align_bytes=64, tag="hs", name="hs")
+            nc.vector.quantize_mx(out=c[:].bitcast(FP8X4), scales=s[:], in_=st["hg", i][:])
+            st["hc", i], st["hs", i] = c, s
+
+        def mm2(i):
+            po = psum.tile([P, D], F32, tag="po", bufs=1, name="po")
+            for g in range(2):
+                rows = slice(P * g, P * g + P)
+                nc.tensor.matmul_mx(
+                    out=po[:],
+                    lhsT=st["hc", i][:, rows].bitcast(FP8X4),
+                    lhsT_scale=st["hs", i][:, rows],
+                    rhs=w2c[:, g, :].bitcast(FP8X4),
+                    rhs_scale=w2sc[:, g, :],
+                    start=(g == 0),
+                    stop=(g == 1),
+                )
+            st["po", i] = po
+
+        def bias_out(i):
+            o = work.tile([P, D], F32, tag="o", name="o")
+            nc.vector.tensor_tensor(out=o[:], in0=st["po", i][:], in1=b2b[:], op=ALU.add)
+            st["o", i] = o
+
+        def slots(i):
+            for half in range(2):
+                ot = outp.tile([P, 4, D], F32, tag="ot", name="ot")
+                for jj in range(4):
+                    j = 4 * half + jj
+                    nc.scalar.activation(
+                        out=ot[:, jj, :], in_=st["o", i][:], func=ACT.Copy, scale=valid[:, i, j : j + 1]
+                    )
+                nc.sync.dma_start(out=out[P * i : P * i + P, 4 * half : 4 * half + 4, :], in_=ot[:])
+
+        for part in range(4):
+            pool(0, part)
+        quant_w1(0)
+        scale_mean(0)
+        quant_w1(1)
+        quant_mean(0)
+        gab = spread(gac, F, "gab")
+        beb = spread(bec, F, "beb")
+        b2b = spread(b2c, D, "b2b")
+        pn = psum.tile([P, 8], F32, tag="po", bufs=1, name="pn")
+        nc.tensor.matmul(out=pn[:], lhsT=nl[:].rearrange("p q i -> p (q i)"), rhs=sel[:], start=True, stop=True)
+        nrow = keep.tile([P, NT], F32)
+        nc.vector.tensor_copy(out=nrow[:], in_=pn[:])
+        valid = keep.tile([P, NT, T], F32)
+        nc.vector.tensor_tensor(
+            out=valid[:],
+            in0=jidx[:].unsqueeze(1).to_broadcast([P, NT, T]),
+            in1=nrow[:].unsqueeze(2).to_broadcast([P, NT, T]),
+            op=ALU.is_lt,
+        )
+        widen_w2(0)
+        mm1(0)
+        bias_gelu(0)
+        widen_w2(1)
+        inter_w2(0)
+        quant_w2(0)
+        inter_w2(1)
+        quant_w2(1)
+
+        for part in range(4):
+            pool(1, part)
+        for s in range(1, NT + 2):
+            nxt = s + 1 if s + 1 < NT else None
+            if s < NT:
+                scale_mean(s)
+            if nxt is not None:
+                pool(nxt, 0)
+            if s >= 2:
+                bias_out(s - 2)
+            if s + 3 < NT:
+                load_ctx(s + 3)
+            if s >= 2:
+                slots(s - 2)
+            if s - 1 < NT:
+                stats(s - 1)
+            if s < NT:
+                quant_mean(s)
+                mm1(s)
+            if nxt is not None:
+                pool(nxt, 1)
+            if s - 1 < NT:
+                norm(s - 1)
+                turn(s - 1)
+            if nxt is not None:
+                pool(nxt, 2)
+            if s < NT:
+                bias_gelu(s)
+            if s - 1 < NT:
+                quant_hn(s - 1)
+                mm2(s - 1)
+            if nxt is not None:
+                pool(nxt, 3)

@@ -68,12 +68,11 @@ def tile_simplepredictor_t_kernel(
                 nc.sync.dma_start(out=t[:], in_=ctx_rows[:, c0 : c0 + HC, :])
                 ctx_tiles[(i, half)] = t
 
-        load_ctx(0)
         w2b = keep.tile([P, 2, 4, 512], U8)
         nc.sync.dma_start(
             out=w2b[:].rearrange("p g j n -> p g (j n)"), in_=W2_bytes.rearrange("(g p j) n -> p g (j n)", g=2, j=4)
         )
-        for i in range(1, 4):
+        for i in range(4):
             load_ctx(i)
 
         identf = keep.tile([P, P], F32)
@@ -142,9 +141,10 @@ def tile_simplepredictor_t_kernel(
         w1g = []
         for n in range(2):
             g = keep.tile([P, 512, 4], BF16, align_bytes=64, name="w1g%d" % n)
-            eng_copy = nc.vector.tensor_copy if n == 0 else nc.scalar.copy
-            eng_copy(out=g[:], in_=w1raw[n][:].rearrange("p j c -> p c j"))
             w1g.append(g)
+
+        def inter_w1(n):
+            nc.vector.tensor_copy(out=w1g[n][:], in_=w1raw[n][:].rearrange("p j c -> p c j"))
 
         def quant_w1(n):
             cols = slice(512 * n, 512 * n + 512)
@@ -256,6 +256,10 @@ def tile_simplepredictor_t_kernel(
             for g in range(2):
                 for u in range(2):
                     nc.tensor.transpose(xt[:, 2 * g + u, :], words[:, 256 * g + u : 256 * g + 256 : 2], identf[:])
+            st["xt", i] = xt
+
+        def turn_copy(i):
+            xt = st["xt", i]
             hg = work.tile([P, 2 * P * 4], BF16, align_bytes=64, tag="hg", name="hg")
             nc.scalar.copy(
                 out=hg[:].bitcast(F32).rearrange("p (g r u) -> p g r u", g=2, u=2),
@@ -289,22 +293,18 @@ def tile_simplepredictor_t_kernel(
             nc.vector.tensor_tensor(out=o[:], in0=st["po", i][:], in1=b2b[:], op=ALU.add)
             st["o", i] = o
 
-        def slots(i):
-            for half in range(2):
-                ot = outp.tile([P, 4, D], F32, tag="ot", name="ot")
-                for jj in range(4):
-                    j = 4 * half + jj
-                    nc.scalar.activation(
-                        out=ot[:, jj, :], in_=st["o", i][:], func=ACT.Copy, scale=valid[:, i, j : j + 1]
-                    )
-                nc.sync.dma_start(out=out[P * i : P * i + P, 4 * half : 4 * half + 4, :], in_=ot[:])
+        def slots(i, on_vector, per):
+            for part in range(T // per):
+                ot = outp.tile([P, per, D], F32, tag="ot", name="ot")
+                for jj in range(per):
+                    j = per * part + jj
+                    m = valid[:, i, j : j + 1]
+                    if j in on_vector:
+                        nc.vector.tensor_scalar_mul(ot[:, jj, :], st["o", i][:], m)
+                    else:
+                        nc.scalar.activation(out=ot[:, jj, :], in_=st["o", i][:], func=ACT.Copy, scale=m)
+                nc.sync.dma_start(out=out[P * i : P * i + P, per * part : per * part + per, :], in_=ot[:])
 
-        for part in range(4):
-            pool(0, part)
-        quant_w1(0)
-        scale_mean(0)
-        quant_w1(1)
-        quant_mean(0)
         gab = spread(gac, F, "gab")
         beb = spread(bec, F, "beb")
         b2b = spread(b2c, D, "b2b")
@@ -319,45 +319,61 @@ def tile_simplepredictor_t_kernel(
             in1=nrow[:].unsqueeze(2).to_broadcast([P, NT, T]),
             op=ALU.is_lt,
         )
+        inter_w1(0)
+        inter_w1(1)
+        quant_w1(0)
+        quant_w1(1)
         widen_w2(0)
-        mm1(0)
-        bias_gelu(0)
         widen_w2(1)
+        for part in range(4):
+            pool(0, part)
         inter_w2(0)
+        scale_mean(0)
         quant_w2(0)
+        quant_mean(0)
+        mm1(0)
         inter_w2(1)
+        bias_gelu(0)
         quant_w2(1)
 
-        for part in range(4):
-            pool(1, part)
-        for s in range(1, NT + 2):
-            nxt = s + 1 if s + 1 < NT else None
-            if s < NT:
-                scale_mean(s)
-            if nxt is not None:
-                pool(nxt, 0)
-            if s >= 2:
-                bias_out(s - 2)
-            if s + 3 < NT:
-                load_ctx(s + 3)
-            if s >= 2:
-                slots(s - 2)
-            if s - 1 < NT:
-                stats(s - 1)
-            if s < NT:
-                quant_mean(s)
-                mm1(s)
-            if nxt is not None:
-                pool(nxt, 1)
-            if s - 1 < NT:
-                norm(s - 1)
-                turn(s - 1)
-            if nxt is not None:
-                pool(nxt, 2)
-            if s < NT:
-                bias_gelu(s)
-            if s - 1 < NT:
-                quant_hn(s - 1)
-                mm2(s - 1)
-            if nxt is not None:
-                pool(nxt, 3)
+        for s in range(1, NT + 3):
+            first = s == 1
+            cur, b, c, d = s, s - 1, s - 2, s - 3
+            if first:
+                for part in range(4):
+                    pool(1, part)
+            if cur < NT:
+                scale_mean(cur)
+            if cur + 3 < NT:
+                load_ctx(cur + 3)
+            if 0 <= d < NT - 2:
+                slots(d, (), 4)
+            if 0 <= c < NT:
+                quant_hn(c)
+            if cur + 1 < NT:
+                pool(cur + 1, 0)
+            if 0 <= c < NT:
+                mm2(c)
+            if d == NT - 2:
+                slots(d, (1, 3, 5), 4)
+            if d == NT - 1:
+                slots(d, (1, 3, 5, 6, 7), 2)
+            if b < NT:
+                stats(b)
+            if cur < NT:
+                quant_mean(cur)
+            if cur + 1 < NT:
+                pool(cur + 1, 1)
+            if cur < NT:
+                mm1(cur)
+            if cur + 1 < NT:
+                pool(cur + 1, 2)
+                pool(cur + 1, 3)
+            if b < NT:
+                norm(b)
+                turn(b)
+                turn_copy(b)
+            if cur < NT:
+                bias_gelu(cur)
+            if 0 <= c < NT:
+                bias_out(c)

@@ -11,6 +11,7 @@ FLOPS = 2 * B * D * F * 2
 P = 128
 NT = B // P
 HC = 8
+PAIRED = 4
 
 F32 = mybir.dt.float32
 BF16 = mybir.dt.bfloat16
@@ -31,41 +32,44 @@ def tile_simplepredictor_t_kernel(
         keep = es.enter_context(tc.tile_pool(name="keep", bufs=1))
         ctxp = es.enter_context(tc.tile_pool(name="ctxp", bufs=8))
         work = es.enter_context(tc.tile_pool(name="work", bufs=2))
-        outp = es.enter_context(tc.tile_pool(name="outp", bufs=8))
+        outp = es.enter_context(tc.tile_pool(name="outp", bufs=4))
         psum = es.enter_context(tc.psum_pool(name="psum", bufs=2))
 
         es.enter_context(tc.manual_schedule())
 
+        def load_cols(vec, per, name):
+            t = keep.tile([P, per], BF16, name=name)
+            nc.scalar.dma_start(out=t[:], in_=vec.rearrange("(p i) -> p i", i=per))
+            return t
+
         cmask = keep.tile([P, 8, L], BF16)
         nc.scalar.dma_start(out=cmask[:], in_=context_mask.rearrange("(p i) l -> p i l", i=8))
-        tmask = keep.tile([P, 8, L], BF16)
-        nc.scalar.dma_start(out=tmask[:], in_=target_mask.rearrange("(p i) l -> p i l", i=8))
-        b1c = keep.tile([P, 8], BF16)
-        nc.scalar.dma_start(out=b1c[:], in_=b1.rearrange("(p i) -> p i", i=8))
-        gac = keep.tile([P, 8], BF16)
-        nc.scalar.dma_start(out=gac[:], in_=gamma.rearrange("(p i) -> p i", i=8))
-        bec = keep.tile([P, 8], BF16)
-        nc.scalar.dma_start(out=bec[:], in_=beta.rearrange("(p i) -> p i", i=8))
-        b2c = keep.tile([P, 4], BF16)
-        nc.scalar.dma_start(out=b2c[:], in_=b2.rearrange("(p i) -> p i", i=4))
+        b1c = load_cols(b1, 8, "b1c")
         w2s = keep.tile([P, 2, 4], F32)
         nc.scalar.dma_start(out=w2s[:], in_=W2_scale.rearrange("(g p j) o -> p g (j o)", g=2, j=4))
+        gac = load_cols(gamma, 8, "gac")
+        bec = load_cols(beta, 8, "bec")
+        b2c = load_cols(b2, 4, "b2c")
+        tmask = keep.tile([P, 8, L], BF16)
+        nc.scalar.dma_start(out=tmask[:], in_=target_mask.rearrange("(p i) l -> p i l", i=8))
 
         w1view = W1.rearrange("(p j) c -> p j c", j=4)
-        w1raw = []
-        for n in range(2):
-            raw = keep.tile([P, 4, 512], BF16, name="w1raw%d" % n)
-            nc.sync.dma_start(out=raw[:], in_=w1view[:, :, 512 * n : 512 * n + 512])
-            w1raw.append(raw)
+        w1raw = keep.tile([P, 4, F], BF16)
+        nc.sync.dma_start(out=w1raw[:], in_=w1view)
 
-        ctx_rows = context_repr.rearrange("b l d -> (b l) d").rearrange("(c p) d -> p c d", p=P)
+        rows = context_repr.rearrange("b l d -> (b l) d")
         ctx_tiles = {}
 
+        def rows_per_part(i):
+            return 2 if i < PAIRED else 1
+
         def load_ctx(i):
+            r = rows_per_part(i)
+            view = rows[2048 * i : 2048 * i + 2048, :].rearrange("(c p r) d -> p c (r d)", p=P, r=r)
+            n = HC // r
             for half in range(2):
-                t = ctxp.tile([P, HC, D], BF16, tag="ctx", name="ctx")
-                c0 = 16 * i + HC * half
-                nc.sync.dma_start(out=t[:], in_=ctx_rows[:, c0 : c0 + HC, :])
+                t = ctxp.tile([P, n, r * D], BF16, tag="ctx", name="ctx")
+                nc.sync.dma_start(out=t[:], in_=view[:, n * half : n * half + n, :])
                 ctx_tiles[(i, half)] = t
 
         w2b = keep.tile([P, 2, 4, 512], U8)
@@ -92,35 +96,30 @@ def tile_simplepredictor_t_kernel(
         sel = keep.tile([P, 8], BF16)
         nc.vector.tensor_reduce(out=self_f[:], in_=identf[:].rearrange("p (g q) -> p g q", q=16), axis=X, op=ALU.add)
         nc.vector.tensor_copy(out=sel[:], in_=self_f[:])
+        sel2_f = keep.tile([P, 16], F32)
+        sel2 = keep.tile([P, 16], BF16)
+        nc.vector.tensor_reduce(out=sel2_f[:], in_=identf[:].rearrange("p (g q) -> p g q", q=8), axis=X, op=ALU.add)
+        nc.vector.tensor_copy(out=sel2[:], in_=sel2_f[:])
+        sels = {1: sel, 2: sel2}
         modq = keep.tile([P, 16], F32)
         nc.vector.tensor_reduce(out=modq[:], in_=identf[:].rearrange("p (g q) -> p q g", q=16), axis=X, op=ALU.add)
 
         cnt = keep.tile([P, 8], F32)
-        nc.vector.tensor_reduce(out=cnt[:], in_=cmask[:], axis=X, op=ALU.add)
         cmax = keep.tile([P, 8], F32)
-        nc.vector.tensor_scalar_max(cmax[:], cnt[:], 1.0)
         crec = keep.tile([P, 8], F32)
-        nc.vector.reciprocal(crec[:], cmax[:])
         rcp = keep.tile([P, 8], F32)
-        nc.vector.scalar_tensor_tensor(out=rcp[:], in0=cnt[:], scalar=0.0, in1=crec[:], op0=ALU.is_gt, op1=ALU.mult)
-
         n8 = keep.tile([P, 8], F32)
-        nc.vector.tensor_reduce(out=n8[:], in_=tmask[:], axis=X, op=ALU.add)
         nl = keep.tile([P, 16, 8], BF16)
-        nc.vector.tensor_tensor(
-            out=nl[:],
-            in0=n8[:].unsqueeze(1).to_broadcast([P, 16, 8]),
-            in1=modq[:].unsqueeze(2).to_broadcast([P, 16, 8]),
-            op=ALU.mult,
-        )
-
         rcpb = keep.tile([P, B], F32)
-        for k in range(2):
+        nrow = keep.tile([P, NT], F32)
+        valid = keep.tile([P, NT, T], F32)
+
+        def rcp_cols(k):
             pr = psum.tile([P, 4, P], F32, tag="h", bufs=4, name="pr")
             for i in range(4):
                 col = rcp[:, 4 * k + i : 4 * k + i + 1]
                 nc.tensor.transpose(pr[:, i, :], col.to_broadcast([P, P]), identf[:])
-            nc.scalar.copy(
+            nc.vector.tensor_copy(
                 out=rcpb[:].rearrange("p (n i) -> p n i", i=8)[:, :, 4 * k : 4 * k + 4],
                 in_=pr[:].rearrange("p i n -> p n i"),
             )
@@ -134,8 +133,6 @@ def tile_simplepredictor_t_kernel(
             nc.scalar.copy(out=dst[:].rearrange("p (n i) -> p n i", i=per), in_=pv[:].rearrange("p i n -> p n i"))
             return dst
 
-        b1b = spread(b1c, F, "b1b")
-
         w1c = keep.tile([P, F], U32, align_bytes=64)
         w1s = keep.tile([P, F], U8, align_bytes=64)
         w1g = []
@@ -144,7 +141,7 @@ def tile_simplepredictor_t_kernel(
             w1g.append(g)
 
         def inter_w1(n):
-            nc.vector.tensor_copy(out=w1g[n][:], in_=w1raw[n][:].rearrange("p j c -> p c j"))
+            nc.vector.tensor_copy(out=w1g[n][:], in_=w1raw[:, :, 512 * n : 512 * n + 512].rearrange("p j c -> p c j"))
 
         def quant_w1(n):
             cols = slice(512 * n, 512 * n + 512)
@@ -177,12 +174,20 @@ def tile_simplepredictor_t_kernel(
             if part == 0:
                 st["ps", i] = psum.tile([P, 4, P], F32, tag="pool", name="ps")
             ps = st["ps", i]
-            for c in range(4 * part, 4 * part + 4):
-                x = ctx_tiles[(i, c // HC)]
+            r = rows_per_part(i)
+            n = HC // r
+            w = 8 * r
+            for c in range(4 * part // r, (4 * part + 4) // r):
+                x = ctx_tiles[(i, c // n)]
                 for t in range(4):
-                    nc.tensor.matmul(
-                        out=ps[:, t, 8 * c : 8 * c + 8], lhsT=x[:, c % HC, t:D:4], rhs=sel[:], start=True, stop=True
-                    )
+                    for e in range(r):
+                        nc.tensor.matmul(
+                            out=ps[:, t, w * c : w * c + w],
+                            lhsT=x[:, c % n, D * e + t : D * e + D : 4],
+                            rhs=sels[r][:],
+                            start=(e == 0),
+                            stop=(e == r - 1),
+                        )
 
         def scale_mean(i):
             m = work.tile([P, P, 4], BF16, align_bytes=64, tag="mean", name="mean")
@@ -218,35 +223,40 @@ def tile_simplepredictor_t_kernel(
                 )
                 st["ph", i].append(ph)
 
-        def bias_gelu(i):
-            v = work.tile([P, F], F32, tag="v", name="v")
-            h = work.tile([P, F], F32, tag="h", name="h")
-            for n in range(2):
-                cols = slice(512 * n, 512 * n + 512)
-                nc.vector.tensor_tensor(out=v[:, cols], in0=st["ph", i][n][:], in1=b1b[:, cols], op=ALU.add)
-                nc.scalar.activation(out=h[:, cols], in_=v[:, cols], func=ACT.Gelu)
-            st["h", i] = h
+        def bias_gelu(i, n):
+            if n == 0:
+                st["v", i] = work.tile([P, F], F32, tag="v", name="v")
+                st["h", i] = work.tile([P, F], F32, tag="h", name="h")
+            v, h = st["v", i], st["h", i]
+            cols = slice(512 * n, 512 * n + 512)
+            nc.vector.tensor_tensor(out=v[:, cols], in0=st["ph", i][n][:], in1=b1b[:, cols], op=ALU.add)
+            nc.scalar.activation(out=h[:, cols], in_=v[:, cols], func=ACT.Gelu)
 
-        def stats(i):
-            bs = work.tile([P, 2, 6], F32, tag="bs", name="bs")
-            for n in range(2):
-                nc.vector.bn_stats(out=bs[:, n, :], in_=st["h", i][:, 512 * n : 512 * n + 512])
+        def stats_part(i, n):
+            if n == 0:
+                st["bs", i] = work.tile([P, 2, 6], F32, tag="bs", name="bs")
+            nc.vector.bn_stats(out=st["bs", i][:, n, :], in_=st["h", i][:, 512 * n : 512 * n + 512])
+
+        def stats_end(i):
             mv = work.tile([P, 2], F32, tag="mv", name="mv")
-            nc.vector.bn_aggr(out=mv[:], in_=bs[:].rearrange("p n s -> p (n s)"))
+            nc.vector.bn_aggr(out=mv[:], in_=st["bs", i][:].rearrange("p n s -> p (n s)"))
             ve = work.tile([P, 1], F32, tag="ve", name="ve")
             nc.gpsimd.tensor_scalar_add(ve[:], mv[:, 1:2], LN_EPS)
             rs = work.tile([P, 1], F32, tag="rs", name="rs")
             nc.gpsimd.tensor_tensor(out=rs[:], in0=ve[:], in1=neghalf[:], op=ALU.pow)
             st["mv", i], st["rs", i] = mv, rs
 
-        def norm(i):
+        def norm_a(i):
             t1 = work.tile([P, F], F32, tag="t1", name="t1")
             nc.vector.scalar_tensor_tensor(
                 out=t1[:], in0=st["h", i][:], scalar=st["mv", i][:, 0:1], in1=gab[:], op0=ALU.subtract, op1=ALU.mult
             )
+            st["t1", i] = t1
+
+        def norm_b(i):
             hn = work.tile([P, F], BF16, tag="hn", name="hn")
             nc.vector.scalar_tensor_tensor(
-                out=hn[:], in0=t1[:], scalar=st["rs", i][:], in1=beb[:], op0=ALU.mult, op1=ALU.add
+                out=hn[:], in0=st["t1", i][:], scalar=st["rs", i][:], in1=beb[:], op0=ALU.mult, op1=ALU.add
             )
             st["hn", i] = hn
 
@@ -293,87 +303,120 @@ def tile_simplepredictor_t_kernel(
             nc.vector.tensor_tensor(out=o[:], in0=st["po", i][:], in1=b2b[:], op=ALU.add)
             st["o", i] = o
 
-        def slots(i, on_vector, per):
-            for part in range(T // per):
-                ot = outp.tile([P, per, D], F32, tag="ot", name="ot")
-                for jj in range(per):
-                    j = per * part + jj
-                    m = valid[:, i, j : j + 1]
-                    if j in on_vector:
-                        nc.vector.tensor_scalar_mul(ot[:, jj, :], st["o", i][:], m)
-                    else:
-                        nc.scalar.activation(out=ot[:, jj, :], in_=st["o", i][:], func=ACT.Copy, scale=m)
-                nc.sync.dma_start(out=out[P * i : P * i + P, per * part : per * part + per, :], in_=ot[:])
+        def slots(i, js, on_vector):
+            if js[0] == 0:
+                st["ot", i] = outp.tile([P, T, D], F32, tag="ot", name="ot")
+            ot = st["ot", i]
+            for j in js:
+                m = valid[:, i, j : j + 1]
+                if j in on_vector:
+                    nc.vector.tensor_scalar_mul(ot[:, j, :], st["o", i][:], m)
+                else:
+                    nc.scalar.activation(out=ot[:, j, :], in_=st["o", i][:], func=ACT.Copy, scale=m)
 
+        def store(i, js):
+            nc.sync.dma_start(
+                out=out[P * i : P * i + P, js[0] : js[0] + len(js), :], in_=st["ot", i][:, js[0] : js[0] + len(js), :]
+            )
+
+        LO, HI = (0, 1, 2, 3), (4, 5, 6, 7)
+
+        b1b = spread(b1c, F, "b1b")
+        widen_w2(0)
         gab = spread(gac, F, "gab")
+        widen_w2(1)
         beb = spread(bec, F, "beb")
         b2b = spread(b2c, D, "b2b")
-        pn = psum.tile([P, 8], F32, tag="po", bufs=1, name="pn")
-        nc.tensor.matmul(out=pn[:], lhsT=nl[:].rearrange("p q i -> p (q i)"), rhs=sel[:], start=True, stop=True)
-        nrow = keep.tile([P, NT], F32)
-        nc.vector.tensor_copy(out=nrow[:], in_=pn[:])
-        valid = keep.tile([P, NT, T], F32)
-        nc.vector.tensor_tensor(
-            out=valid[:],
-            in0=jidx[:].unsqueeze(1).to_broadcast([P, NT, T]),
-            in1=nrow[:].unsqueeze(2).to_broadcast([P, NT, T]),
-            op=ALU.is_lt,
-        )
         inter_w1(0)
         inter_w1(1)
+        nc.vector.tensor_reduce(out=cnt[:], in_=cmask[:], axis=X, op=ALU.add)
         quant_w1(0)
+        nc.vector.tensor_scalar_max(cmax[:], cnt[:], 1.0)
         quant_w1(1)
-        widen_w2(0)
-        widen_w2(1)
+        nc.vector.reciprocal(crec[:], cmax[:])
+        nc.vector.tensor_reduce(out=n8[:], in_=tmask[:], axis=X, op=ALU.add)
+        nc.vector.scalar_tensor_tensor(out=rcp[:], in0=cnt[:], scalar=0.0, in1=crec[:], op0=ALU.is_gt, op1=ALU.mult)
+        nc.vector.tensor_tensor(
+            out=nl[:],
+            in0=n8[:].unsqueeze(1).to_broadcast([P, 16, 8]),
+            in1=modq[:].unsqueeze(2).to_broadcast([P, 16, 8]),
+            op=ALU.mult,
+        )
+        rcp_cols(0)
+        rcp_cols(1)
+        pn = psum.tile([P, 8], F32, tag="po", bufs=1, name="pn")
+        nc.tensor.matmul(out=pn[:], lhsT=nl[:].rearrange("p q i -> p (q i)"), rhs=sel[:], start=True, stop=True)
+        nc.vector.tensor_copy(out=nrow[:], in_=pn[:])
         for part in range(4):
             pool(0, part)
-        inter_w2(0)
+        load_ctx(4)
         scale_mean(0)
-        quant_w2(0)
+        inter_w2(0)
         quant_mean(0)
         mm1(0)
-        inter_w2(1)
-        bias_gelu(0)
-        quant_w2(1)
+        quant_w2(0)
 
-        for s in range(1, NT + 3):
-            first = s == 1
-            cur, b, c, d = s, s - 1, s - 2, s - 3
-            if first:
-                for part in range(4):
-                    pool(1, part)
+        for s in range(NT + 2):
+            cur, b, c, d, nxt = s, s - 1, s - 2, s - 3, s + 1
+            if 0 < s and cur + 4 < NT:
+                load_ctx(cur + 4)
+            if 0 <= c < NT:
+                turn_copy(c)
+            if 0 <= d < NT:
+                slots(d, HI, (5, 7) if d == NT - 2 else ())
+                if d < NT - 2:
+                    store(d, LO + HI)
+                else:
+                    store(d, HI)
+            if nxt < NT:
+                if s == 0:
+                    pool(nxt, 0)
+                    pool(nxt, 1)
+                pool(nxt, 2)
+                pool(nxt, 3)
+            if 0 <= b < NT:
+                stats_part(b, 0)
+                stats_part(b, 1)
             if cur < NT:
-                scale_mean(cur)
-            if cur + 3 < NT:
-                load_ctx(cur + 3)
-            if 0 <= d < NT - 2:
-                slots(d, (), 4)
+                bias_gelu(cur, 0)
+            if 0 <= b < NT:
+                stats_end(b)
             if 0 <= c < NT:
                 quant_hn(c)
-            if cur + 1 < NT:
-                pool(cur + 1, 0)
-            if 0 <= c < NT:
                 mm2(c)
-            if d == NT - 2:
-                slots(d, (1, 3, 5), 4)
-            if d == NT - 1:
-                slots(d, (1, 3, 5, 6, 7), 2)
-            if b < NT:
-                stats(b)
+            if 2 <= s < NT - 2:
+                pool(s + 2, 0)
+                pool(s + 2, 1)
             if cur < NT:
-                quant_mean(cur)
-            if cur + 1 < NT:
-                pool(cur + 1, 1)
-            if cur < NT:
-                mm1(cur)
-            if cur + 1 < NT:
-                pool(cur + 1, 2)
-                pool(cur + 1, 3)
-            if b < NT:
-                norm(b)
-                turn(b)
-                turn_copy(b)
-            if cur < NT:
-                bias_gelu(cur)
+                bias_gelu(cur, 1)
+            if 0 <= b < NT:
+                norm_a(b)
             if 0 <= c < NT:
                 bias_out(c)
+                if c < NT - 1:
+                    slots(c, LO, ())
+                    if c == NT - 2:
+                        store(c, LO)
+            if s == 0:
+                inter_w2(1)
+                nc.vector.tensor_tensor(
+                    out=valid[:],
+                    in0=jidx[:].unsqueeze(1).to_broadcast([P, NT, T]),
+                    in1=nrow[:].unsqueeze(2).to_broadcast([P, NT, T]),
+                    op=ALU.is_lt,
+                )
+                quant_w2(1)
+            if nxt < NT:
+                scale_mean(nxt)
+            if 0 <= b < NT:
+                norm_b(b)
+                turn(b)
+            if nxt < NT:
+                quant_mean(nxt)
+                mm1(nxt)
+            if s < 2:
+                pool(s + 2, 0)
+                pool(s + 2, 1)
+        for js, on_vector in (((0, 1), (1,)), ((2, 3), (3,)), ((4, 5), (5,)), ((6, 7), (6, 7))):
+            slots(NT - 1, js, on_vector)
+            store(NT - 1, js)

@@ -10,8 +10,8 @@ LN_EPS = 1e-5
 FLOPS = 2 * B * D * F * 2
 P = 128
 NT = B // P
-HC = 8
-PAIRED = 4
+HC = 4
+PAIRED = 19
 
 F32 = mybir.dt.float32
 BF16 = mybir.dt.bfloat16
@@ -30,7 +30,7 @@ def tile_simplepredictor_t_kernel(
     nc = tc.nc
     with ExitStack() as es:
         keep = es.enter_context(tc.tile_pool(name="keep", bufs=1))
-        ctxp = es.enter_context(tc.tile_pool(name="ctxp", bufs=8))
+        ctxp = es.enter_context(tc.tile_pool(name="ctxp", bufs=16))
         work = es.enter_context(tc.tile_pool(name="work", bufs=2))
         outp = es.enter_context(tc.tile_pool(name="outp", bufs=4))
         psum = es.enter_context(tc.psum_pool(name="psum", bufs=2))
@@ -60,23 +60,25 @@ def tile_simplepredictor_t_kernel(
         rows = context_repr.rearrange("b l d -> (b l) d")
         ctx_tiles = {}
 
-        def rows_per_part(i):
-            return 2 if i < PAIRED else 1
+        def rows_per_part(i, part):
+            return 2 if 4 * i + part < PAIRED else 1
 
         def load_ctx(i):
-            r = rows_per_part(i)
-            view = rows[2048 * i : 2048 * i + 2048, :].rearrange("(c p r) d -> p c (r d)", p=P, r=r)
-            n = HC // r
-            for half in range(2):
-                t = ctxp.tile([P, n, r * D], BF16, tag="ctx", name="ctx")
-                nc.sync.dma_start(out=t[:], in_=view[:, n * half : n * half + n, :])
-                ctx_tiles[(i, half)] = t
+            for part in range(4):
+                r = rows_per_part(i, part)
+                k = 4 * i + part
+                t = ctxp.tile([P, HC // r, r * D], BF16, tag="ctx", name="ctx")
+                nc.sync.dma_start(
+                    out=t[:], in_=rows[512 * k : 512 * k + 512, :].rearrange("(c p r) d -> p c (r d)", p=P, r=r)
+                )
+                ctx_tiles[(i, part)] = t
 
+        load_ctx(0)
         w2b = keep.tile([P, 2, 4, 512], U8)
         nc.sync.dma_start(
             out=w2b[:].rearrange("p g j n -> p g (j n)"), in_=W2_bytes.rearrange("(g p j) n -> p g (j n)", g=2, j=4)
         )
-        for i in range(4):
+        for i in range(1, 4):
             load_ctx(i)
 
         identf = keep.tile([P, P], F32)
@@ -95,7 +97,6 @@ def tile_simplepredictor_t_kernel(
         self_f = keep.tile([P, 8], F32)
         sel = keep.tile([P, 8], BF16)
         nc.vector.tensor_reduce(out=self_f[:], in_=identf[:].rearrange("p (g q) -> p g q", q=16), axis=X, op=ALU.add)
-        nc.vector.tensor_copy(out=sel[:], in_=self_f[:])
         sel2_f = keep.tile([P, 16], F32)
         sel2 = keep.tile([P, 16], BF16)
         nc.vector.tensor_reduce(out=sel2_f[:], in_=identf[:].rearrange("p (g q) -> p g q", q=8), axis=X, op=ALU.add)
@@ -141,7 +142,7 @@ def tile_simplepredictor_t_kernel(
             w1g.append(g)
 
         def inter_w1(n):
-            nc.vector.tensor_copy(out=w1g[n][:], in_=w1raw[:, :, 512 * n : 512 * n + 512].rearrange("p j c -> p c j"))
+            (nc.scalar.copy if n == 1 else nc.vector.tensor_copy)(out=w1g[n][:], in_=w1raw[:, :, 512 * n : 512 * n + 512].rearrange("p j c -> p c j"))
 
         def quant_w1(n):
             cols = slice(512 * n, 512 * n + 512)
@@ -161,7 +162,7 @@ def tile_simplepredictor_t_kernel(
                 )
 
         def inter_w2(g):
-            nc.vector.tensor_copy(out=w2g[g][:], in_=w2w[:, g].rearrange("p j n -> p n j"))
+            (nc.scalar.copy if g in (0, 1) else nc.vector.tensor_copy)(out=w2g[g][:], in_=w2w[:, g].rearrange("p j n -> p n j"))
 
         def quant_w2(g):
             nc.vector.quantize_mx(
@@ -174,16 +175,16 @@ def tile_simplepredictor_t_kernel(
             if part == 0:
                 st["ps", i] = psum.tile([P, 4, P], F32, tag="pool", name="ps")
             ps = st["ps", i]
-            r = rows_per_part(i)
-            n = HC // r
+            r = rows_per_part(i, part)
             w = 8 * r
-            for c in range(4 * part // r, (4 * part + 4) // r):
-                x = ctx_tiles[(i, c // n)]
+            x = ctx_tiles[(i, part)]
+            for c in range(HC // r):
+                b0 = 32 * part + w * c
                 for t in range(4):
                     for e in range(r):
                         nc.tensor.matmul(
-                            out=ps[:, t, w * c : w * c + w],
-                            lhsT=x[:, c % n, D * e + t : D * e + D : 4],
+                            out=ps[:, t, b0 : b0 + w],
+                            lhsT=x[:, c, D * e + t : D * e + D : 4],
                             rhs=sels[r][:],
                             start=(e == 0),
                             stop=(e == r - 1),
@@ -321,40 +322,34 @@ def tile_simplepredictor_t_kernel(
 
         LO, HI = (0, 1, 2, 3), (4, 5, 6, 7)
 
+        nc.vector.tensor_reduce(out=cnt[:], in_=cmask[:], axis=X, op=ALU.add)
+        nc.vector.tensor_scalar_max(cmax[:], cnt[:], 1.0)
+        nc.vector.reciprocal(crec[:], cmax[:])
+        nc.vector.scalar_tensor_tensor(out=rcp[:], in0=cnt[:], scalar=0.0, in1=crec[:], op0=ALU.is_gt, op1=ALU.mult)
         b1b = spread(b1c, F, "b1b")
-        widen_w2(0)
-        gab = spread(gac, F, "gab")
-        widen_w2(1)
-        beb = spread(bec, F, "beb")
-        b2b = spread(b2c, D, "b2b")
         inter_w1(0)
         inter_w1(1)
-        nc.vector.tensor_reduce(out=cnt[:], in_=cmask[:], axis=X, op=ALU.add)
+        rcp_cols(0)
+        pool(0, 0)
+        rcp_cols(1)
+        pool(0, 1)
+        pool(0, 2)
+        pool(0, 3)
         quant_w1(0)
-        nc.vector.tensor_scalar_max(cmax[:], cnt[:], 1.0)
         quant_w1(1)
-        nc.vector.reciprocal(crec[:], cmax[:])
+        load_ctx(4)
+        scale_mean(0)
         nc.vector.tensor_reduce(out=n8[:], in_=tmask[:], axis=X, op=ALU.add)
-        nc.vector.scalar_tensor_tensor(out=rcp[:], in0=cnt[:], scalar=0.0, in1=crec[:], op0=ALU.is_gt, op1=ALU.mult)
+        nc.vector.tensor_copy(out=sel[:], in_=self_f[:])
+        quant_mean(0)
+        mm1(0)
         nc.vector.tensor_tensor(
             out=nl[:],
             in0=n8[:].unsqueeze(1).to_broadcast([P, 16, 8]),
             in1=modq[:].unsqueeze(2).to_broadcast([P, 16, 8]),
             op=ALU.mult,
         )
-        rcp_cols(0)
-        rcp_cols(1)
-        pn = psum.tile([P, 8], F32, tag="po", bufs=1, name="pn")
-        nc.tensor.matmul(out=pn[:], lhsT=nl[:].rearrange("p q i -> p (q i)"), rhs=sel[:], start=True, stop=True)
-        nc.vector.tensor_copy(out=nrow[:], in_=pn[:])
-        for part in range(4):
-            pool(0, part)
-        load_ctx(4)
-        scale_mean(0)
-        inter_w2(0)
-        quant_mean(0)
-        mm1(0)
-        quant_w2(0)
+        widen_w2(0)
 
         for s in range(NT + 2):
             cur, b, c, d, nxt = s, s - 1, s - 2, s - 3, s + 1
@@ -364,59 +359,74 @@ def tile_simplepredictor_t_kernel(
                 turn_copy(c)
             if 0 <= d < NT:
                 slots(d, HI, (5, 7) if d == NT - 2 else ())
-                if d < NT - 2:
-                    store(d, LO + HI)
-                else:
-                    store(d, HI)
+                store(d, LO + HI if d < 4 else HI)
             if nxt < NT:
                 if s == 0:
-                    pool(nxt, 0)
-                    pool(nxt, 1)
+                    pool(1, 0)
+                    pool(1, 1)
                 pool(nxt, 2)
-                pool(nxt, 3)
+                if s != 2:
+                    pool(nxt, 3)
             if 0 <= b < NT:
                 stats_part(b, 0)
                 stats_part(b, 1)
             if cur < NT:
                 bias_gelu(cur, 0)
-            if 0 <= b < NT:
+            if 0 <= b < NT - 1:
                 stats_end(b)
+            if s == 2:
+                quant_w2(1)
             if 0 <= c < NT:
                 quant_hn(c)
                 mm2(c)
-            if 2 <= s < NT - 2:
+            if b == NT - 1:
+                stats_end(b)
+            if s == 2:
+                pool(3, 3)
+            if 1 <= s < NT - 2:
                 pool(s + 2, 0)
                 pool(s + 2, 1)
             if cur < NT:
                 bias_gelu(cur, 1)
+            if s == 0:
+                inter_w2(0)
+                gab = spread(gac, F, "gab")
+                beb = spread(bec, F, "beb")
+                widen_w2(1)
+                pn = psum.tile([P, 8], F32, tag="po", bufs=1, name="pn")
+                nc.tensor.matmul(out=pn[:], lhsT=nl[:].rearrange("p q i -> p (q i)"), rhs=sel[:], start=True, stop=True)
+            if s == 1:
+                nc.vector.tensor_copy(out=nrow[:], in_=pn[:])
+                inter_w2(1)
+                b2b = spread(b2c, D, "b2b")
+                quant_w2(0)
             if 0 <= b < NT:
                 norm_a(b)
             if 0 <= c < NT:
                 bias_out(c)
                 if c < NT - 1:
                     slots(c, LO, ())
-                    if c == NT - 2:
+                    if c >= 4:
                         store(c, LO)
-            if s == 0:
-                inter_w2(1)
+            if nxt < NT:
+                scale_mean(nxt)
+            if s == 1:
                 nc.vector.tensor_tensor(
                     out=valid[:],
                     in0=jidx[:].unsqueeze(1).to_broadcast([P, NT, T]),
                     in1=nrow[:].unsqueeze(2).to_broadcast([P, NT, T]),
                     op=ALU.is_lt,
                 )
-                quant_w2(1)
-            if nxt < NT:
-                scale_mean(nxt)
+            if s == 0:
+                pool(2, 0)
             if 0 <= b < NT:
                 norm_b(b)
                 turn(b)
             if nxt < NT:
                 quant_mean(nxt)
                 mm1(nxt)
-            if s < 2:
-                pool(s + 2, 0)
-                pool(s + 2, 1)
+            if s == 0:
+                pool(2, 1)
         for js, on_vector in (((0, 1), (1,)), ((2, 3), (3,)), ((4, 5), (5,)), ((6, 7), (6, 7))):
             slots(NT - 1, js, on_vector)
             store(NT - 1, js)

@@ -7,11 +7,22 @@ B, L, D, T = 1024, 16, 512, 8
 F = 2 * D
 LN_EPS = 1e-5
 
-FLOPS = 2 * B * D * F * 2
+FLOPS = 2 * B * D * F + 2 * B * F * D
+
 P = 128
 NT = B // P
-HC = 4
-PAIRED = 19
+LAST = NT - 1
+HALF = F // 2
+QUARTERS = 4
+BLOCKS = 4
+
+PAIRED_QUARTERS = 19
+
+QUARTERS_PER_LOAD = (1, 1, 1, 2, 4, 4, 4, 4)
+
+FIRST_HALF_STORED = 3
+
+LOW, HIGH = (0, 1, 2, 3), (4, 5, 6, 7)
 
 F32 = mybir.dt.float32
 BF16 = mybir.dt.bfloat16
@@ -24,409 +35,465 @@ ACT = mybir.ActivationFunctionType
 X = mybir.AxisListType.X
 
 
+def rows_per_partition(i, quarter):
+    return 2 if QUARTERS * i + quarter < PAIRED_QUARTERS else 1
+
+
+def hidden_block(g, u):
+    c0 = HALF * g + 256 * u
+    return slice(c0, c0 + 256)
+
+
 def tile_simplepredictor_t_kernel(
     tc, context_repr, target_mask, context_mask, W1, b1, gamma, beta, W2_bytes, W2_scale, b2, num_targets, out
 ):
     nc = tc.nc
+    assert num_targets == T
     with ExitStack() as es:
         keep = es.enter_context(tc.tile_pool(name="keep", bufs=1))
-        ctxp = es.enter_context(tc.tile_pool(name="ctxp", bufs=16))
+        ctxp = es.enter_context(tc.tile_pool(name="ctxp", bufs=4))
         work = es.enter_context(tc.tile_pool(name="work", bufs=2))
         outp = es.enter_context(tc.tile_pool(name="outp", bufs=4))
         psum = es.enter_context(tc.psum_pool(name="psum", bufs=2))
 
         es.enter_context(tc.manual_schedule())
 
-        def load_cols(vec, per, name):
-            t = keep.tile([P, per], BF16, name=name)
-            nc.scalar.dma_start(out=t[:], in_=vec.rearrange("(p i) -> p i", i=per))
-            return t
+        def load_vector(vec, per, name):
+            cols = keep.tile([P, per], BF16, name=name)
+            nc.scalar.dma_start(out=cols[:], in_=vec.rearrange("(p i) -> p i", i=per))
+            return cols
 
         cmask = keep.tile([P, 8, L], BF16)
         nc.scalar.dma_start(out=cmask[:], in_=context_mask.rearrange("(p i) l -> p i l", i=8))
-        b1c = load_cols(b1, 8, "b1c")
-        w2s = keep.tile([P, 2, 4], F32)
-        nc.scalar.dma_start(out=w2s[:], in_=W2_scale.rearrange("(g p j) o -> p g (j o)", g=2, j=4))
-        gac = load_cols(gamma, 8, "gac")
-        bec = load_cols(beta, 8, "bec")
-        b2c = load_cols(b2, 4, "b2c")
+        b1_cols = load_vector(b1, 8, "b1_cols")
+        w2_scale = keep.tile([P, 2, 4], F32)
+        nc.scalar.dma_start(out=w2_scale[:], in_=W2_scale.rearrange("(g p t) o -> p g (t o)", g=2, t=4))
+        gamma_cols = load_vector(gamma, 8, "gamma_cols")
+        beta_cols = load_vector(beta, 8, "beta_cols")
+        b2_cols = load_vector(b2, 4, "b2_cols")
         tmask = keep.tile([P, 8, L], BF16)
         nc.scalar.dma_start(out=tmask[:], in_=target_mask.rearrange("(p i) l -> p i l", i=8))
 
-        w1view = W1.rearrange("(p j) c -> p j c", j=4)
-        w1raw = keep.tile([P, 4, F], BF16)
-        nc.sync.dma_start(out=w1raw[:], in_=w1view)
+        w1_rows = keep.tile([P, 4, F], BF16)
+        nc.sync.dma_start(out=w1_rows[:], in_=W1.rearrange("(p t) c -> p t c", t=4))
 
         rows = context_repr.rearrange("b l d -> (b l) d")
-        ctx_tiles = {}
+        ctx = {}
 
-        def rows_per_part(i, part):
-            return 2 if 4 * i + part < PAIRED else 1
-
-        def load_ctx(i):
-            for part in range(4):
-                r = rows_per_part(i, part)
-                k = 4 * i + part
-                t = ctxp.tile([P, HC // r, r * D], BF16, tag="ctx", name="ctx")
+        def load_rows(i):
+            ctx[i] = ctxp.tile([P, QUARTERS, BLOCKS, D], BF16, tag="ctx", name="ctx")
+            q = 0
+            while q < QUARTERS:
+                r = rows_per_partition(i, q)
+                n = 1
+                while n < QUARTERS_PER_LOAD[i] and q + n < QUARTERS and rows_per_partition(i, q + n) == r:
+                    n += 1
+                row0 = 512 * (QUARTERS * i + q)
                 nc.sync.dma_start(
-                    out=t[:], in_=rows[512 * k : 512 * k + 512, :].rearrange("(c p r) d -> p c (r d)", p=P, r=r)
+                    out=ctx[i][:, q : q + n].rearrange("p q (c r) d -> p (q c) (r d)", r=r),
+                    in_=rows[row0 : row0 + 512 * n, :].rearrange("(c p r) d -> p c (r d)", p=P, r=r),
                 )
-                ctx_tiles[(i, part)] = t
+                q += n
 
-        load_ctx(0)
-        w2b = keep.tile([P, 2, 4, 512], U8)
+        load_rows(0)
+        w2_bytes = keep.tile([P, 2, 4, D], U8)
         nc.sync.dma_start(
-            out=w2b[:].rearrange("p g j n -> p g (j n)"), in_=W2_bytes.rearrange("(g p j) n -> p g (j n)", g=2, j=4)
+            out=w2_bytes[:].rearrange("p g t n -> p g (t n)"), in_=W2_bytes.rearrange("(g p t) n -> p g (t n)", g=2, t=4)
         )
         for i in range(1, 4):
-            load_ctx(i)
+            load_rows(i)
 
-        identf = keep.tile([P, P], F32)
-        make_identity(nc, identf[:])
-        neghalf = keep.tile([P, 1], F32)
-        nc.gpsimd.memset(neghalf[:], -0.5)
-        jidx = keep.tile([P, T], F32)
-        nc.gpsimd.iota(jidx[:], pattern=[[1, T]], base=0, channel_multiplier=0, allow_small_or_imprecise_dtypes=True)
-        warm = keep.tile([P, 1], F32)
-        nc.gpsimd.memset(warm[:], 0.0)
-        warm2 = keep.tile([P, 1], F32)
-        nc.scalar.activation(out=warm2[:], in_=warm[:], func=ACT.Gelu)
+        ident_f32 = keep.tile([P, P], F32)
+        make_identity(nc, ident_f32[:])
+        minus_half = keep.tile([P, 1], F32)
+        nc.gpsimd.memset(minus_half[:], -0.5)
+        slot_index = keep.tile([P, T], F32)
+        nc.gpsimd.iota(
+            slot_index[:], pattern=[[1, T]], base=0, channel_multiplier=0, allow_small_or_imprecise_dtypes=True
+        )
+        table_in = keep.tile([P, 1], F32)
+        nc.gpsimd.memset(table_in[:], 0.0)
+        table_out = keep.tile([P, 1], F32)
+        nc.scalar.activation(out=table_out[:], in_=table_in[:], func=ACT.Gelu)
 
-        identb = keep.tile([P, P], BF16)
-        nc.vector.tensor_copy(out=identb[:], in_=identf[:])
-        self_f = keep.tile([P, 8], F32)
-        sel = keep.tile([P, 8], BF16)
-        nc.vector.tensor_reduce(out=self_f[:], in_=identf[:].rearrange("p (g q) -> p g q", q=16), axis=X, op=ALU.add)
-        sel2_f = keep.tile([P, 16], F32)
+        ident_bf16 = keep.tile([P, P], BF16)
+        nc.vector.tensor_copy(out=ident_bf16[:], in_=ident_f32[:])
+        sel2_f32 = keep.tile([P, 16], F32)
         sel2 = keep.tile([P, 16], BF16)
-        nc.vector.tensor_reduce(out=sel2_f[:], in_=identf[:].rearrange("p (g q) -> p g q", q=8), axis=X, op=ALU.add)
-        nc.vector.tensor_copy(out=sel2[:], in_=sel2_f[:])
-        sels = {1: sel, 2: sel2}
-        modq = keep.tile([P, 16], F32)
-        nc.vector.tensor_reduce(out=modq[:], in_=identf[:].rearrange("p (g q) -> p q g", q=16), axis=X, op=ALU.add)
+        nc.vector.tensor_reduce(out=sel2_f32[:], in_=ident_f32[:].rearrange("p (j q) -> p j q", q=8), axis=X, op=ALU.add)
+        nc.vector.tensor_copy(out=sel2[:], in_=sel2_f32[:])
+        sel1_f32 = keep.tile([P, 8], F32)
+        sel1 = keep.tile([P, 8], BF16)
+        nc.vector.tensor_reduce(out=sel1_f32[:], in_=ident_f32[:].rearrange("p (j q) -> p j q", q=16), axis=X, op=ALU.add)
+        pooling = {1: sel1, 2: sel2}
+        mod16 = keep.tile([P, 16], F32)
+        nc.vector.tensor_reduce(out=mod16[:], in_=ident_f32[:].rearrange("p (j q) -> p q j", q=16), axis=X, op=ALU.add)
 
-        cnt = keep.tile([P, 8], F32)
-        cmax = keep.tile([P, 8], F32)
-        crec = keep.tile([P, 8], F32)
-        rcp = keep.tile([P, 8], F32)
-        n8 = keep.tile([P, 8], F32)
-        nl = keep.tile([P, 16, 8], BF16)
-        rcpb = keep.tile([P, B], F32)
-        nrow = keep.tile([P, NT], F32)
-        valid = keep.tile([P, NT, T], F32)
+        count = keep.tile([P, 8], F32)
+        count_or_1 = keep.tile([P, 8], F32)
+        reciprocal = keep.tile([P, 8], F32)
+        factor = keep.tile([P, 8], F32)
+        factor_all = keep.tile([P, B], F32)
 
-        def rcp_cols(k):
-            pr = psum.tile([P, 4, P], F32, tag="h", bufs=4, name="pr")
+        def spread_factor(k):
+            turned = psum.tile([P, 4, P], F32, tag="h", bufs=4, name="turned")
             for i in range(4):
-                col = rcp[:, 4 * k + i : 4 * k + i + 1]
-                nc.tensor.transpose(pr[:, i, :], col.to_broadcast([P, P]), identf[:])
+                column = factor[:, 4 * k + i : 4 * k + i + 1]
+                nc.tensor.transpose(turned[:, i, :], column.to_broadcast([P, P]), ident_f32[:])
             nc.vector.tensor_copy(
-                out=rcpb[:].rearrange("p (n i) -> p n i", i=8)[:, :, 4 * k : 4 * k + 4],
-                in_=pr[:].rearrange("p i n -> p n i"),
+                out=factor_all[:].rearrange("p (n i) -> p n i", i=8)[:, :, 4 * k : 4 * k + 4],
+                in_=turned[:].rearrange("p i n -> p n i"),
             )
 
-        def spread(col, width, name):
-            per = width // P
-            dst = keep.tile([P, width], BF16, name=name)
-            pv = psum.tile([P, per, P], BF16, tag="h", bufs=4, name="pv")
+        def turn_vector(cols, per):
+            turned = psum.tile([P, per, P], BF16, tag="h", bufs=4, name="turned")
             for i in range(per):
-                nc.tensor.transpose(pv[:, i, :], col[:, i : i + 1].to_broadcast([P, P]), identb[:])
-            nc.scalar.copy(out=dst[:].rearrange("p (n i) -> p n i", i=per), in_=pv[:].rearrange("p i n -> p n i"))
+                nc.tensor.transpose(turned[:, i, :], cols[:, i : i + 1].to_broadcast([P, P]), ident_bf16[:])
+            return turned
+
+        def spread_hidden(cols, name):
+            dst = keep.tile([P, F], BF16, name=name)
+            src = turn_vector(cols, 8)[:].rearrange("p (v u e) n -> p u n v e", u=2, e=2)
+            for g in range(2):
+                for u in range(2):
+                    nc.scalar.copy(
+                        out=dst[:, hidden_block(g, u)].rearrange("p (n v e) -> p n v e", v=2, e=2),
+                        in_=src[:, u, 64 * g : 64 * g + 64],
+                    )
             return dst
 
-        w1c = keep.tile([P, F], U32, align_bytes=64)
-        w1s = keep.tile([P, F], U8, align_bytes=64)
-        w1g = []
-        for n in range(2):
-            g = keep.tile([P, 512, 4], BF16, align_bytes=64, name="w1g%d" % n)
-            w1g.append(g)
+        w1_codes = keep.tile([P, F], U32, align_bytes=64)
+        w1_planes = keep.tile([P, F], U8, align_bytes=64)
+        w1_words = [keep.tile([P, HALF, 4], BF16, align_bytes=64, name="w1_words%d" % g) for g in range(2)]
 
-        def inter_w1(n):
-            (nc.scalar.copy if n == 1 else nc.vector.tensor_copy)(out=w1g[n][:], in_=w1raw[:, :, 512 * n : 512 * n + 512].rearrange("p j c -> p c j"))
+        def interleave_w1(g):
+            copy = (nc.vector.tensor_copy, nc.scalar.copy)[g]
+            src = w1_rows[:, :, HALF * g : HALF * g + HALF].rearrange("p t (m u e) -> p u m e t", u=2, e=2)
+            for u in range(2):
+                copy(out=w1_words[g][:, hidden_block(0, u), :].rearrange("p (m e) t -> p m e t", e=2), in_=src[:, u])
 
-        def quant_w1(n):
-            cols = slice(512 * n, 512 * n + 512)
+        def quantise_w1(g):
+            cols = slice(HALF * g, HALF * g + HALF)
             nc.vector.quantize_mx(
-                out=w1c[:, cols].bitcast(FP8X4), scales=w1s[:, cols], in_=w1g[n][:].rearrange("p c j -> p (c j)")
+                out=w1_codes[:, cols].bitcast(FP8X4),
+                scales=w1_planes[:, cols],
+                in_=w1_words[g][:].rearrange("p c t -> p (c t)"),
             )
 
-        w2w = keep.tile([P, 2, 4, 512], BF16)
-        w2g = [keep.tile([P, 512, 4], BF16, align_bytes=64, name="w2g%d" % g) for g in range(2)]
-        w2c = keep.tile([P, 2, 512], U32, align_bytes=64)
-        w2sc = keep.tile([P, 2, 512], U8, align_bytes=64)
+        w2_rows = keep.tile([P, 2, 4, D], BF16)
+        w2_words = [keep.tile([P, D, 4], BF16, align_bytes=64, name="w2_words%d" % g) for g in range(2)]
+        w2_codes = keep.tile([P, 2, D], U32, align_bytes=64)
+        w2_planes = keep.tile([P, 2, D], U8, align_bytes=64)
 
         def widen_w2(g):
-            for j in range(4):
+            for t in range(4):
                 nc.scalar.activation(
-                    out=w2w[:, g, j, :], in_=w2b[:, g, j, :].bitcast(FP8), func=ACT.Copy, scale=w2s[:, g, j : j + 1]
+                    out=w2_rows[:, g, t, :],
+                    in_=w2_bytes[:, g, t, :].bitcast(FP8),
+                    func=ACT.Copy,
+                    scale=w2_scale[:, g, t : t + 1],
                 )
 
-        def inter_w2(g):
-            (nc.scalar.copy if g in (0, 1) else nc.vector.tensor_copy)(out=w2g[g][:], in_=w2w[:, g].rearrange("p j n -> p n j"))
+        def interleave_w2(g):
+            nc.scalar.copy(out=w2_words[g][:], in_=w2_rows[:, g].rearrange("p t n -> p n t"))
 
-        def quant_w2(g):
+        def quantise_w2(g):
             nc.vector.quantize_mx(
-                out=w2c[:, g, :].bitcast(FP8X4), scales=w2sc[:, g, :], in_=w2g[g][:].rearrange("p n j -> p (n j)")
+                out=w2_codes[:, g, :].bitcast(FP8X4),
+                scales=w2_planes[:, g, :],
+                in_=w2_words[g][:].rearrange("p n t -> p (n t)"),
             )
 
         st = {}
 
-        def pool(i, part):
-            if part == 0:
-                st["ps", i] = psum.tile([P, 4, P], F32, tag="pool", name="ps")
-            ps = st["ps", i]
-            r = rows_per_part(i, part)
-            w = 8 * r
-            x = ctx_tiles[(i, part)]
-            for c in range(HC // r):
-                b0 = 32 * part + w * c
+        def pool(i, q):
+            if q == 0:
+                st["sums", i] = psum.tile([P, 4, P], F32, tag="pool", name="sums")
+            r = rows_per_partition(i, q)
+            width = 8 * r
+            x = ctx[i][:, q].rearrange("p (c r) d -> p c (r d)", r=r)
+            for c in range(BLOCKS // r):
+                b0 = 32 * q + width * c
                 for t in range(4):
                     for e in range(r):
                         nc.tensor.matmul(
-                            out=ps[:, t, b0 : b0 + w],
+                            out=st["sums", i][:, t, b0 : b0 + width],
                             lhsT=x[:, c, D * e + t : D * e + D : 4],
-                            rhs=sels[r][:],
+                            rhs=pooling[r][:],
                             start=(e == 0),
                             stop=(e == r - 1),
                         )
 
         def scale_mean(i):
-            m = work.tile([P, P, 4], BF16, align_bytes=64, tag="mean", name="mean")
+            mean = work.tile([P, P, 4], BF16, align_bytes=64, tag="mean", name="mean")
             nc.vector.tensor_tensor(
-                out=m[:],
-                in0=st["ps", i][:].rearrange("p t b -> p b t"),
-                in1=rcpb[:, P * i : P * i + P].unsqueeze(2).to_broadcast([P, P, 4]),
+                out=mean[:],
+                in0=st["sums", i][:].rearrange("p t b -> p b t"),
+                in1=factor_all[:, P * i : P * i + P].unsqueeze(2).to_broadcast([P, P, 4]),
                 op=ALU.mult,
             )
-            st["mean", i] = m
+            st["mean", i] = mean
 
-        def quant_mean(i):
-            c = work.tile([P, P], U32, align_bytes=64, tag="mc", name="mc")
-            s = work.tile([P, P], U8, align_bytes=64, tag="ms", name="ms")
+        def quantise_mean(i):
+            codes = work.tile([P, P], U32, align_bytes=64, tag="mean_codes", name="mean_codes")
+            plane = work.tile([P, P], U8, align_bytes=64, tag="mean_plane", name="mean_plane")
             nc.vector.quantize_mx(
-                out=c[:].bitcast(FP8X4), scales=s[:], in_=st["mean", i][:].rearrange("p b t -> p (b t)")
+                out=codes[:].bitcast(FP8X4), scales=plane[:], in_=st["mean", i][:].rearrange("p b t -> p (b t)")
             )
-            st["mc", i], st["ms", i] = c, s
+            st["mean_codes", i], st["mean_plane", i] = codes, plane
 
-        def mm1(i):
-            st["ph", i] = []
-            for n in range(2):
-                ph = psum.tile([P, 512], F32, tag="h", bufs=4, name="ph")
-                cols = slice(512 * n, 512 * n + 512)
+        def multiply_w1(i):
+            for g in range(2):
+                cols = slice(HALF * g, HALF * g + HALF)
+                acc = psum.tile([P, HALF], F32, tag="h", bufs=4, name="acc")
                 nc.tensor.matmul_mx(
-                    out=ph[:],
-                    lhsT=st["mc", i][:].bitcast(FP8X4),
-                    lhsT_scale=st["ms", i][:],
-                    rhs=w1c[:, cols].bitcast(FP8X4),
-                    rhs_scale=w1s[:, cols],
+                    out=acc[:],
+                    lhsT=st["mean_codes", i][:].bitcast(FP8X4),
+                    lhsT_scale=st["mean_plane", i][:],
+                    rhs=w1_codes[:, cols].bitcast(FP8X4),
+                    rhs_scale=w1_planes[:, cols],
                     start=True,
                     stop=True,
                 )
-                st["ph", i].append(ph)
+                st["acc", i, g] = acc
 
-        def bias_gelu(i, n):
-            if n == 0:
+        def bias_and_gelu(i, g):
+            if g == 0:
                 st["v", i] = work.tile([P, F], F32, tag="v", name="v")
                 st["h", i] = work.tile([P, F], F32, tag="h", name="h")
-            v, h = st["v", i], st["h", i]
-            cols = slice(512 * n, 512 * n + 512)
-            nc.vector.tensor_tensor(out=v[:, cols], in0=st["ph", i][n][:], in1=b1b[:, cols], op=ALU.add)
-            nc.scalar.activation(out=h[:, cols], in_=v[:, cols], func=ACT.Gelu)
+            cols = slice(HALF * g, HALF * g + HALF)
+            v = st["v", i][:, cols]
+            nc.vector.tensor_tensor(out=v, in0=st["acc", i, g][:], in1=b1_all[:, cols], op=ALU.add)
+            nc.scalar.activation(out=st["h", i][:, cols], in_=v, func=ACT.Gelu)
 
-        def stats_part(i, n):
-            if n == 0:
-                st["bs", i] = work.tile([P, 2, 6], F32, tag="bs", name="bs")
-            nc.vector.bn_stats(out=st["bs", i][:, n, :], in_=st["h", i][:, 512 * n : 512 * n + 512])
+        def half_statistics(i, g):
+            if g == 0:
+                st["half_stats", i] = work.tile([P, 2, 6], F32, tag="half_stats", name="half_stats")
+            nc.vector.bn_stats(out=st["half_stats", i][:, g, :], in_=st["h", i][:, HALF * g : HALF * g + HALF])
 
-        def stats_end(i):
-            mv = work.tile([P, 2], F32, tag="mv", name="mv")
-            nc.vector.bn_aggr(out=mv[:], in_=st["bs", i][:].rearrange("p n s -> p (n s)"))
-            ve = work.tile([P, 1], F32, tag="ve", name="ve")
-            nc.gpsimd.tensor_scalar_add(ve[:], mv[:, 1:2], LN_EPS)
-            rs = work.tile([P, 1], F32, tag="rs", name="rs")
-            nc.gpsimd.tensor_tensor(out=rs[:], in0=ve[:], in1=neghalf[:], op=ALU.pow)
-            st["mv", i], st["rs", i] = mv, rs
+        def statistics(i):
+            stats = work.tile([P, 2], F32, tag="stats", name="stats")
+            nc.vector.bn_aggr(out=stats[:], in_=st["half_stats", i][:].rearrange("p g s -> p (g s)"))
+            var_eps = work.tile([P, 1], F32, tag="var_eps", name="var_eps")
+            nc.gpsimd.tensor_scalar_add(var_eps[:], stats[:, 1:2], LN_EPS)
+            rstd = work.tile([P, 1], F32, tag="rstd", name="rstd")
+            nc.gpsimd.tensor_tensor(out=rstd[:], in0=var_eps[:], in1=minus_half[:], op=ALU.pow)
+            st["stats", i], st["rstd", i] = stats, rstd
 
-        def norm_a(i):
-            t1 = work.tile([P, F], F32, tag="t1", name="t1")
+        def centre(i):
+            centred = work.tile([P, F], F32, tag="centred", name="centred")
             nc.vector.scalar_tensor_tensor(
-                out=t1[:], in0=st["h", i][:], scalar=st["mv", i][:, 0:1], in1=gab[:], op0=ALU.subtract, op1=ALU.mult
+                out=centred[:],
+                in0=st["h", i][:],
+                scalar=st["stats", i][:, 0:1],
+                in1=gamma_all[:],
+                op0=ALU.subtract,
+                op1=ALU.mult,
             )
-            st["t1", i] = t1
+            st["centred", i] = centred
 
-        def norm_b(i):
+        def normalise(i):
             hn = work.tile([P, F], BF16, tag="hn", name="hn")
             nc.vector.scalar_tensor_tensor(
-                out=hn[:], in0=st["t1", i][:], scalar=st["rs", i][:], in1=beb[:], op0=ALU.mult, op1=ALU.add
+                out=hn[:], in0=st["centred", i][:], scalar=st["rstd", i][:], in1=beta_all[:], op0=ALU.mult, op1=ALU.add
             )
             st["hn", i] = hn
 
-        def turn(i):
-            xt = psum.tile([P, 4, P], F32, tag="xt", bufs=1, name="xt")
+        def transpose_hn(i):
+            turned = psum.tile([P, 2, 2, P], F32, tag="turned_hn", bufs=1, name="turned_hn")
             words = st["hn", i][:].bitcast(F32)
             for g in range(2):
                 for u in range(2):
-                    nc.tensor.transpose(xt[:, 2 * g + u, :], words[:, 256 * g + u : 256 * g + 256 : 2], identf[:])
-            st["xt", i] = xt
+                    w0 = 256 * g + 128 * u
+                    nc.tensor.transpose(turned[:, g, u, :], words[:, w0 : w0 + 128], ident_f32[:])
+            st["turned_hn", i] = turned
 
-        def turn_copy(i):
-            xt = st["xt", i]
-            hg = work.tile([P, 2 * P * 4], BF16, align_bytes=64, tag="hg", name="hg")
+        def interleave_hn(i):
+            hn_words = work.tile([P, 2 * P * 4], BF16, align_bytes=64, tag="hn_words", name="hn_words")
             nc.scalar.copy(
-                out=hg[:].bitcast(F32).rearrange("p (g r u) -> p g r u", g=2, u=2),
-                in_=xt[:].rearrange("p (g u) r -> p g r u", g=2),
+                out=hn_words[:].bitcast(F32).rearrange("p (g b u) -> p g b u", g=2, u=2),
+                in_=st["turned_hn", i][:].rearrange("p g u b -> p g b u"),
             )
-            st["hg", i] = hg
+            st["hn_words", i] = hn_words
 
-        def quant_hn(i):
-            c = work.tile([P, 2 * P], U32, align_bytes=64, tag="hc", name="hc")
-            s = work.tile([P, 2 * P], U8, align_bytes=64, tag="hs", name="hs")
-            nc.vector.quantize_mx(out=c[:].bitcast(FP8X4), scales=s[:], in_=st["hg", i][:])
-            st["hc", i], st["hs", i] = c, s
+        def quantise_hn(i):
+            codes = work.tile([P, 2 * P], U32, align_bytes=64, tag="hn_codes", name="hn_codes")
+            plane = work.tile([P, 2 * P], U8, align_bytes=64, tag="hn_plane", name="hn_plane")
+            nc.vector.quantize_mx(out=codes[:].bitcast(FP8X4), scales=plane[:], in_=st["hn_words", i][:])
+            st["hn_codes", i], st["hn_plane", i] = codes, plane
 
-        def mm2(i):
-            po = psum.tile([P, D], F32, tag="po", bufs=1, name="po")
+        def multiply_w2(i):
+            acc = psum.tile([P, D], F32, tag="out", bufs=1, name="acc2")
             for g in range(2):
-                rows = slice(P * g, P * g + P)
+                part = slice(P * g, P * g + P)
                 nc.tensor.matmul_mx(
-                    out=po[:],
-                    lhsT=st["hc", i][:, rows].bitcast(FP8X4),
-                    lhsT_scale=st["hs", i][:, rows],
-                    rhs=w2c[:, g, :].bitcast(FP8X4),
-                    rhs_scale=w2sc[:, g, :],
+                    out=acc[:],
+                    lhsT=st["hn_codes", i][:, part].bitcast(FP8X4),
+                    lhsT_scale=st["hn_plane", i][:, part],
+                    rhs=w2_codes[:, g, :].bitcast(FP8X4),
+                    rhs_scale=w2_planes[:, g, :],
                     start=(g == 0),
                     stop=(g == 1),
                 )
-            st["po", i] = po
+            st["acc2", i] = acc
 
-        def bias_out(i):
-            o = work.tile([P, D], F32, tag="o", name="o")
-            nc.vector.tensor_tensor(out=o[:], in0=st["po", i][:], in1=b2b[:], op=ALU.add)
-            st["o", i] = o
+        def add_b2(i):
+            prediction = work.tile([P, D], F32, tag="prediction", name="prediction")
+            nc.vector.tensor_tensor(out=prediction[:], in0=st["acc2", i][:], in1=b2_all[:], op=ALU.add)
+            st["prediction", i] = prediction
 
-        def slots(i, js, on_vector):
-            if js[0] == 0:
-                st["ot", i] = outp.tile([P, T, D], F32, tag="ot", name="ot")
-            ot = st["ot", i]
-            for j in js:
-                m = valid[:, i, j : j + 1]
+        def fill_slots(i, slots, on_vector=()):
+            if slots[0] == 0:
+                st["slots", i] = outp.tile([P, T, D], F32, tag="slots", name="slots")
+            for j in slots:
+                mask = valid[:, i, j : j + 1]
+                dst = st["slots", i][:, j, :]
                 if j in on_vector:
-                    nc.vector.tensor_scalar_mul(ot[:, j, :], st["o", i][:], m)
+                    nc.vector.tensor_scalar_mul(dst, st["prediction", i][:], mask)
                 else:
-                    nc.scalar.activation(out=ot[:, j, :], in_=st["o", i][:], func=ACT.Copy, scale=m)
+                    nc.scalar.activation(out=dst, in_=st["prediction", i][:], func=ACT.Copy, scale=mask)
 
-        def store(i, js):
-            nc.sync.dma_start(
-                out=out[P * i : P * i + P, js[0] : js[0] + len(js), :], in_=st["ot", i][:, js[0] : js[0] + len(js), :]
-            )
+        def store_slots(i, slots):
+            part = slice(slots[0], slots[0] + len(slots))
+            nc.sync.dma_start(out=out[P * i : P * i + P, part, :], in_=st["slots", i][:, part, :])
 
-        LO, HI = (0, 1, 2, 3), (4, 5, 6, 7)
-
-        nc.vector.tensor_reduce(out=cnt[:], in_=cmask[:], axis=X, op=ALU.add)
-        nc.vector.tensor_scalar_max(cmax[:], cnt[:], 1.0)
-        nc.vector.reciprocal(crec[:], cmax[:])
-        nc.vector.scalar_tensor_tensor(out=rcp[:], in0=cnt[:], scalar=0.0, in1=crec[:], op0=ALU.is_gt, op1=ALU.mult)
-        b1b = spread(b1c, F, "b1b")
-        inter_w1(0)
-        inter_w1(1)
-        rcp_cols(0)
+        nc.vector.tensor_reduce(out=count[:], in_=cmask[:], axis=X, op=ALU.add)
+        nc.vector.tensor_scalar_max(count_or_1[:], count[:], 1.0)
+        nc.vector.reciprocal(reciprocal[:], count_or_1[:])
+        nc.vector.scalar_tensor_tensor(
+            out=factor[:], in0=count[:], scalar=0.0, in1=reciprocal[:], op0=ALU.is_gt, op1=ALU.mult
+        )
+        b1_all = spread_hidden(b1_cols, "b1_all")
+        interleave_w1(0)
+        interleave_w1(1)
+        spread_factor(0)
         pool(0, 0)
-        rcp_cols(1)
+        spread_factor(1)
         pool(0, 1)
         pool(0, 2)
         pool(0, 3)
-        quant_w1(0)
-        quant_w1(1)
-        load_ctx(4)
+        quantise_w1(0)
+        quantise_w1(1)
+        load_rows(4)
         scale_mean(0)
-        nc.vector.tensor_reduce(out=n8[:], in_=tmask[:], axis=X, op=ALU.add)
-        nc.vector.tensor_copy(out=sel[:], in_=self_f[:])
-        quant_mean(0)
-        mm1(0)
+
+        target_n = keep.tile([P, 8], F32)
+        nc.vector.tensor_reduce(out=target_n[:], in_=tmask[:], axis=X, op=ALU.add)
+        nc.vector.tensor_copy(out=sel1[:], in_=sel1_f32[:])
+        quantise_mean(0)
+        multiply_w1(0)
+        picked = keep.tile([P, 16, 8], BF16)
         nc.vector.tensor_tensor(
-            out=nl[:],
-            in0=n8[:].unsqueeze(1).to_broadcast([P, 16, 8]),
-            in1=modq[:].unsqueeze(2).to_broadcast([P, 16, 8]),
+            out=picked[:],
+            in0=target_n[:].unsqueeze(1).to_broadcast([P, 16, 8]),
+            in1=mod16[:].unsqueeze(2).to_broadcast([P, 16, 8]),
             op=ALU.mult,
         )
         widen_w2(0)
+        n_of_row = keep.tile([P, NT], F32)
+        valid = keep.tile([P, NT, T], F32)
 
-        for s in range(NT + 2):
-            cur, b, c, d, nxt = s, s - 1, s - 2, s - 3, s + 1
-            if 0 < s and cur + 4 < NT:
-                load_ctx(cur + 4)
-            if 0 <= c < NT:
-                turn_copy(c)
-            if 0 <= d < NT:
-                slots(d, HI, (5, 7) if d == NT - 2 else ())
-                store(d, LO + HI if d < 4 else HI)
+        for s in range(NT):
+            nxt = s + 1
+            if 0 < s < NT - 4:
+                load_rows(s + 4)
+            if s >= 2:
+                interleave_hn(s - 2)
+            if s >= 3:
+                fill_slots(s - 3, HIGH)
+                store_slots(s - 3, LOW + HIGH if s - 3 < FIRST_HALF_STORED else HIGH)
             if nxt < NT:
                 if s == 0:
-                    pool(1, 0)
-                    pool(1, 1)
+                    pool(nxt, 0)
+                    pool(nxt, 1)
                 pool(nxt, 2)
                 if s != 2:
                     pool(nxt, 3)
-            if 0 <= b < NT:
-                stats_part(b, 0)
-                stats_part(b, 1)
-            if cur < NT:
-                bias_gelu(cur, 0)
-            if 0 <= b < NT - 1:
-                stats_end(b)
+            if s >= 1:
+                half_statistics(s - 1, 0)
+                half_statistics(s - 1, 1)
+            bias_and_gelu(s, 0)
+            if s >= 1:
+                statistics(s - 1)
             if s == 2:
-                quant_w2(1)
-            if 0 <= c < NT:
-                quant_hn(c)
-                mm2(c)
-            if b == NT - 1:
-                stats_end(b)
+                quantise_w2(1)
+            if s >= 2:
+                quantise_hn(s - 2)
+                multiply_w2(s - 2)
             if s == 2:
-                pool(3, 3)
+                pool(nxt, 3)
             if 1 <= s < NT - 2:
                 pool(s + 2, 0)
                 pool(s + 2, 1)
-            if cur < NT:
-                bias_gelu(cur, 1)
+            bias_and_gelu(s, 1)
+
             if s == 0:
-                inter_w2(0)
-                gab = spread(gac, F, "gab")
-                beb = spread(bec, F, "beb")
+                interleave_w2(0)
+                gamma_all = spread_hidden(gamma_cols, "gamma_all")
+                beta_all = spread_hidden(beta_cols, "beta_all")
                 widen_w2(1)
-                pn = psum.tile([P, 8], F32, tag="po", bufs=1, name="pn")
-                nc.tensor.matmul(out=pn[:], lhsT=nl[:].rearrange("p q i -> p (q i)"), rhs=sel[:], start=True, stop=True)
+                n_psum = psum.tile([P, NT], F32, tag="out", bufs=1, name="n_psum")
+                nc.tensor.matmul(
+                    out=n_psum[:], lhsT=picked[:].rearrange("p q i -> p (q i)"), rhs=sel1[:], start=True, stop=True
+                )
             if s == 1:
-                nc.vector.tensor_copy(out=nrow[:], in_=pn[:])
-                inter_w2(1)
-                b2b = spread(b2c, D, "b2b")
-                quant_w2(0)
-            if 0 <= b < NT:
-                norm_a(b)
-            if 0 <= c < NT:
-                bias_out(c)
-                if c < NT - 1:
-                    slots(c, LO, ())
-                    if c >= 4:
-                        store(c, LO)
+                nc.vector.tensor_copy(out=n_of_row[:], in_=n_psum[:])
+                interleave_w2(1)
+                b2_all = keep.tile([P, D], BF16)
+                nc.scalar.copy(
+                    out=b2_all[:].rearrange("p (n i) -> p n i", i=4),
+                    in_=turn_vector(b2_cols, 4)[:].rearrange("p i n -> p n i"),
+                )
+                quantise_w2(0)
+
+            if s >= 1:
+                centre(s - 1)
+            if s >= 2:
+                add_b2(s - 2)
+                fill_slots(s - 2, LOW)
+                if s - 2 >= FIRST_HALF_STORED:
+                    store_slots(s - 2, LOW)
             if nxt < NT:
                 scale_mean(nxt)
             if s == 1:
                 nc.vector.tensor_tensor(
                     out=valid[:],
-                    in0=jidx[:].unsqueeze(1).to_broadcast([P, NT, T]),
-                    in1=nrow[:].unsqueeze(2).to_broadcast([P, NT, T]),
+                    in0=slot_index[:].unsqueeze(1).to_broadcast([P, NT, T]),
+                    in1=n_of_row[:].unsqueeze(2).to_broadcast([P, NT, T]),
                     op=ALU.is_lt,
                 )
             if s == 0:
-                pool(2, 0)
-            if 0 <= b < NT:
-                norm_b(b)
-                turn(b)
+                pool(s + 2, 0)
+            if s >= 1:
+                normalise(s - 1)
+                transpose_hn(s - 1)
             if nxt < NT:
-                quant_mean(nxt)
-                mm1(nxt)
+                quantise_mean(nxt)
+                multiply_w1(nxt)
             if s == 0:
-                pool(2, 1)
-        for js, on_vector in (((0, 1), (1,)), ((2, 3), (3,)), ((4, 5), (5,)), ((6, 7), (6, 7))):
-            slots(NT - 1, js, on_vector)
-            store(NT - 1, js)
+                pool(s + 2, 1)
+
+        interleave_hn(LAST - 1)
+        fill_slots(LAST - 2, HIGH)
+        store_slots(LAST - 2, HIGH)
+        half_statistics(LAST, 0)
+        half_statistics(LAST, 1)
+        statistics(LAST)
+        centre(LAST)
+        quantise_hn(LAST - 1)
+        multiply_w2(LAST - 1)
+        normalise(LAST)
+        transpose_hn(LAST)
+        add_b2(LAST - 1)
+        interleave_hn(LAST)
+        fill_slots(LAST - 1, LOW, on_vector=(1, 2, 3))
+        store_slots(LAST - 1, LOW)
+        quantise_hn(LAST)
+        multiply_w2(LAST)
+        fill_slots(LAST - 1, HIGH, on_vector=(6, 7))
+        store_slots(LAST - 1, HIGH)
+        add_b2(LAST)
+        for j in range(0, T, 2):
+            pair = (j, j + 1)
+            fill_slots(LAST, pair, on_vector=pair if j == T - 2 else (j + 1,))
+            store_slots(LAST, pair)

from contextlib import ExitStack

import concourse.mybir as mybir
from concourse.masks import make_identity

B, L, D, T = 1024, 16, 512, 8
F = 2 * D
LN_EPS = 1e-5

FLOPS = 2 * B * D * F + 2 * B * F * D

P = 128
NT = B // P
LAST = NT - 1
HALF = F // 2
QUARTERS = 4
BLOCKS = 4

PAIRED_QUARTERS = 19

QUARTERS_PER_LOAD = (1, 1, 1, 2, 4, 4, 4, 4)

FIRST_HALF_STORED = 3

LOW, HIGH = (0, 1, 2, 3), (4, 5, 6, 7)

F32 = mybir.dt.float32
BF16 = mybir.dt.bfloat16
U32 = mybir.dt.uint32
U8 = mybir.dt.uint8
FP8 = mybir.dt.float8_e4m3fn
FP8X4 = mybir.dt.float8_e4m3fn_x4
ALU = mybir.AluOpType
ACT = mybir.ActivationFunctionType
X = mybir.AxisListType.X


def rows_per_partition(i, quarter):
    return 2 if QUARTERS * i + quarter < PAIRED_QUARTERS else 1


def hidden_block(g, u):
    c0 = HALF * g + 256 * u
    return slice(c0, c0 + 256)


def tile_simplepredictor_t_kernel(
    tc, context_repr, target_mask, context_mask, W1, b1, gamma, beta, W2_bytes, W2_scale, b2, num_targets, out
):
    nc = tc.nc
    assert num_targets == T
    with ExitStack() as es:
        keep = es.enter_context(tc.tile_pool(name="keep", bufs=1))
        ctxp = es.enter_context(tc.tile_pool(name="ctxp", bufs=4))
        work = es.enter_context(tc.tile_pool(name="work", bufs=2))
        outp = es.enter_context(tc.tile_pool(name="outp", bufs=4))
        psum = es.enter_context(tc.psum_pool(name="psum", bufs=2))

        es.enter_context(tc.manual_schedule())

        def load_vector(vec, per, name):
            cols = keep.tile([P, per], BF16, name=name)
            nc.scalar.dma_start(out=cols[:], in_=vec.rearrange("(p i) -> p i", i=per))
            return cols

        cmask = keep.tile([P, 8, L], BF16)
        nc.scalar.dma_start(out=cmask[:], in_=context_mask.rearrange("(p i) l -> p i l", i=8))
        b1_cols = load_vector(b1, 8, "b1_cols")
        w2_scale = keep.tile([P, 2, 4], F32)
        nc.scalar.dma_start(out=w2_scale[:], in_=W2_scale.rearrange("(g p t) o -> p g (t o)", g=2, t=4))
        gamma_cols = load_vector(gamma, 8, "gamma_cols")
        beta_cols = load_vector(beta, 8, "beta_cols")
        b2_cols = load_vector(b2, 4, "b2_cols")
        tmask = keep.tile([P, 8, L], BF16)
        nc.scalar.dma_start(out=tmask[:], in_=target_mask.rearrange("(p i) l -> p i l", i=8))

        w1_rows = keep.tile([P, 4, F], BF16)
        nc.sync.dma_start(out=w1_rows[:], in_=W1.rearrange("(p t) c -> p t c", t=4))

        rows = context_repr.rearrange("b l d -> (b l) d")
        ctx = {}

        def load_rows(i):
            ctx[i] = ctxp.tile([P, QUARTERS, BLOCKS, D], BF16, tag="ctx", name="ctx")
            q = 0
            while q < QUARTERS:
                r = rows_per_partition(i, q)
                n = 1
                while n < QUARTERS_PER_LOAD[i] and q + n < QUARTERS and rows_per_partition(i, q + n) == r:
                    n += 1
                row0 = 512 * (QUARTERS * i + q)
                nc.sync.dma_start(
                    out=ctx[i][:, q : q + n].rearrange("p q (c r) d -> p (q c) (r d)", r=r),
                    in_=rows[row0 : row0 + 512 * n, :].rearrange("(c p r) d -> p c (r d)", p=P, r=r),
                )
                q += n

        load_rows(0)
        w2_bytes = keep.tile([P, 2, 4, D], U8)
        nc.sync.dma_start(
            out=w2_bytes[:].rearrange("p g t n -> p g (t n)"), in_=W2_bytes.rearrange("(g p t) n -> p g (t n)", g=2, t=4)
        )
        for i in range(1, 4):
            load_rows(i)

        ident_f32 = keep.tile([P, P], F32)
        make_identity(nc, ident_f32[:])
        minus_half = keep.tile([P, 1], F32)
        nc.gpsimd.memset(minus_half[:], -0.5)
        slot_index = keep.tile([P, T], F32)
        nc.gpsimd.iota(
            slot_index[:], pattern=[[1, T]], base=0, channel_multiplier=0, allow_small_or_imprecise_dtypes=True
        )
        table_in = keep.tile([P, 1], F32)
        nc.gpsimd.memset(table_in[:], 0.0)
        table_out = keep.tile([P, 1], F32)
        nc.scalar.activation(out=table_out[:], in_=table_in[:], func=ACT.Gelu)

        ident_bf16 = keep.tile([P, P], BF16)
        nc.vector.tensor_copy(out=ident_bf16[:], in_=ident_f32[:])
        sel2_f32 = keep.tile([P, 16], F32)
        sel2 = keep.tile([P, 16], BF16)
        nc.vector.tensor_reduce(out=sel2_f32[:], in_=ident_f32[:].rearrange("p (j q) -> p j q", q=8), axis=X, op=ALU.add)
        nc.vector.tensor_copy(out=sel2[:], in_=sel2_f32[:])
        sel1_f32 = keep.tile([P, 8], F32)
        sel1 = keep.tile([P, 8], BF16)
        nc.vector.tensor_reduce(out=sel1_f32[:], in_=ident_f32[:].rearrange("p (j q) -> p j q", q=16), axis=X, op=ALU.add)
        pooling = {1: sel1, 2: sel2}
        mod16 = keep.tile([P, 16], F32)
        nc.vector.tensor_reduce(out=mod16[:], in_=ident_f32[:].rearrange("p (j q) -> p q j", q=16), axis=X, op=ALU.add)

        count = keep.tile([P, 8], F32)
        count_or_1 = keep.tile([P, 8], F32)
        reciprocal = keep.tile([P, 8], F32)
        factor = keep.tile([P, 8], F32)
        factor_all = keep.tile([P, B], F32)

        def spread_factor(k):
            turned = psum.tile([P, 4, P], F32, tag="h", bufs=4, name="turned")
            for i in range(4):
                column = factor[:, 4 * k + i : 4 * k + i + 1]
                nc.tensor.transpose(turned[:, i, :], column.to_broadcast([P, P]), ident_f32[:])
            nc.vector.tensor_copy(
                out=factor_all[:].rearrange("p (n i) -> p n i", i=8)[:, :, 4 * k : 4 * k + 4],
                in_=turned[:].rearrange("p i n -> p n i"),
            )

        def turn_vector(cols, per):
            turned = psum.tile([P, per, P], BF16, tag="h", bufs=4, name="turned")
            for i in range(per):
                nc.tensor.transpose(turned[:, i, :], cols[:, i : i + 1].to_broadcast([P, P]), ident_bf16[:])
            return turned

        def spread_hidden(cols, name):
            dst = keep.tile([P, F], BF16, name=name)
            src = turn_vector(cols, 8)[:].rearrange("p (v u e) n -> p u n v e", u=2, e=2)
            for g in range(2):
                for u in range(2):
                    nc.scalar.copy(
                        out=dst[:, hidden_block(g, u)].rearrange("p (n v e) -> p n v e", v=2, e=2),
                        in_=src[:, u, 64 * g : 64 * g + 64],
                    )
            return dst

        w1_codes = keep.tile([P, F], U32, align_bytes=64)
        w1_planes = keep.tile([P, F], U8, align_bytes=64)
        w1_words = [keep.tile([P, HALF, 4], BF16, align_bytes=64, name="w1_words%d" % g) for g in range(2)]

        def interleave_w1(g):
            copy = (nc.vector.tensor_copy, nc.scalar.copy)[g]
            src = w1_rows[:, :, HALF * g : HALF * g + HALF].rearrange("p t (m u e) -> p u m e t", u=2, e=2)
            for u in range(2):
                copy(out=w1_words[g][:, hidden_block(0, u), :].rearrange("p (m e) t -> p m e t", e=2), in_=src[:, u])

        def quantise_w1(g):
            cols = slice(HALF * g, HALF * g + HALF)
            nc.vector.quantize_mx(
                out=w1_codes[:, cols].bitcast(FP8X4),
                scales=w1_planes[:, cols],
                in_=w1_words[g][:].rearrange("p c t -> p (c t)"),
            )

        w2_rows = keep.tile([P, 2, 4, D], BF16)
        w2_words = [keep.tile([P, D, 4], BF16, align_bytes=64, name="w2_words%d" % g) for g in range(2)]
        w2_codes = keep.tile([P, 2, D], U32, align_bytes=64)
        w2_planes = keep.tile([P, 2, D], U8, align_bytes=64)

        def widen_w2(g):
            for t in range(4):
                nc.scalar.activation(
                    out=w2_rows[:, g, t, :],
                    in_=w2_bytes[:, g, t, :].bitcast(FP8),
                    func=ACT.Copy,
                    scale=w2_scale[:, g, t : t + 1],
                )

        def interleave_w2(g):
            nc.scalar.copy(out=w2_words[g][:], in_=w2_rows[:, g].rearrange("p t n -> p n t"))

        def quantise_w2(g):
            nc.vector.quantize_mx(
                out=w2_codes[:, g, :].bitcast(FP8X4),
                scales=w2_planes[:, g, :],
                in_=w2_words[g][:].rearrange("p n t -> p (n t)"),
            )

        st = {}

        def pool(i, q):
            if q == 0:
                st["sums", i] = psum.tile([P, 4, P], F32, tag="pool", name="sums")
            r = rows_per_partition(i, q)
            width = 8 * r
            x = ctx[i][:, q].rearrange("p (c r) d -> p c (r d)", r=r)
            for c in range(BLOCKS // r):
                b0 = 32 * q + width * c
                for t in range(4):
                    for e in range(r):
                        nc.tensor.matmul(
                            out=st["sums", i][:, t, b0 : b0 + width],
                            lhsT=x[:, c, D * e + t : D * e + D : 4],
                            rhs=pooling[r][:],
                            start=(e == 0),
                            stop=(e == r - 1),
                        )

        def scale_mean(i):
            mean = work.tile([P, P, 4], BF16, align_bytes=64, tag="mean", name="mean")
            nc.vector.tensor_tensor(
                out=mean[:],
                in0=st["sums", i][:].rearrange("p t b -> p b t"),
                in1=factor_all[:, P * i : P * i + P].unsqueeze(2).to_broadcast([P, P, 4]),
                op=ALU.mult,
            )
            st["mean", i] = mean

        def quantise_mean(i):
            codes = work.tile([P, P], U32, align_bytes=64, tag="mean_codes", name="mean_codes")
            plane = work.tile([P, P], U8, align_bytes=64, tag="mean_plane", name="mean_plane")
            nc.vector.quantize_mx(
                out=codes[:].bitcast(FP8X4), scales=plane[:], in_=st["mean", i][:].rearrange("p b t -> p (b t)")
            )
            st["mean_codes", i], st["mean_plane", i] = codes, plane

        def multiply_w1(i):
            for g in range(2):
                cols = slice(HALF * g, HALF * g + HALF)
                acc = psum.tile([P, HALF], F32, tag="h", bufs=4, name="acc")
                nc.tensor.matmul_mx(
                    out=acc[:],
                    lhsT=st["mean_codes", i][:].bitcast(FP8X4),
                    lhsT_scale=st["mean_plane", i][:],
                    rhs=w1_codes[:, cols].bitcast(FP8X4),
                    rhs_scale=w1_planes[:, cols],
                    start=True,
                    stop=True,
                )
                st["acc", i, g] = acc

        def bias_and_gelu(i, g):
            if g == 0:
                st["v", i] = work.tile([P, F], F32, tag="v", name="v")
                st["h", i] = work.tile([P, F], F32, tag="h", name="h")
            cols = slice(HALF * g, HALF * g + HALF)
            v = st["v", i][:, cols]
            nc.vector.tensor_tensor(out=v, in0=st["acc", i, g][:], in1=b1_all[:, cols], op=ALU.add)
            nc.scalar.activation(out=st["h", i][:, cols], in_=v, func=ACT.Gelu)

        def half_statistics(i, g):
            if g == 0:
                st["half_stats", i] = work.tile([P, 2, 6], F32, tag="half_stats", name="half_stats")
            nc.vector.bn_stats(out=st["half_stats", i][:, g, :], in_=st["h", i][:, HALF * g : HALF * g + HALF])

        def statistics(i):
            stats = work.tile([P, 2], F32, tag="stats", name="stats")
            nc.vector.bn_aggr(out=stats[:], in_=st["half_stats", i][:].rearrange("p g s -> p (g s)"))
            var_eps = work.tile([P, 1], F32, tag="var_eps", name="var_eps")
            nc.gpsimd.tensor_scalar_add(var_eps[:], stats[:, 1:2], LN_EPS)
            rstd = work.tile([P, 1], F32, tag="rstd", name="rstd")
            nc.gpsimd.tensor_tensor(out=rstd[:], in0=var_eps[:], in1=minus_half[:], op=ALU.pow)
            st["stats", i], st["rstd", i] = stats, rstd

        def centre(i):
            centred = work.tile([P, F], F32, tag="centred", name="centred")
            nc.vector.scalar_tensor_tensor(
                out=centred[:],
                in0=st["h", i][:],
                scalar=st["stats", i][:, 0:1],
                in1=gamma_all[:],
                op0=ALU.subtract,
                op1=ALU.mult,
            )
            st["centred", i] = centred

        def normalise(i):
            hn = work.tile([P, F], BF16, tag="hn", name="hn")
            nc.vector.scalar_tensor_tensor(
                out=hn[:], in0=st["centred", i][:], scalar=st["rstd", i][:], in1=beta_all[:], op0=ALU.mult, op1=ALU.add
            )
            st["hn", i] = hn

        def transpose_hn(i):
            turned = psum.tile([P, 2, 2, P], F32, tag="turned_hn", bufs=1, name="turned_hn")
            words = st["hn", i][:].bitcast(F32)
            for g in range(2):
                for u in range(2):
                    w0 = 256 * g + 128 * u
                    nc.tensor.transpose(turned[:, g, u, :], words[:, w0 : w0 + 128], ident_f32[:])
            st["turned_hn", i] = turned

        def interleave_hn(i):
            hn_words = work.tile([P, 2 * P * 4], BF16, align_bytes=64, tag="hn_words", name="hn_words")
            nc.scalar.copy(
                out=hn_words[:].bitcast(F32).rearrange("p (g b u) -> p g b u", g=2, u=2),
                in_=st["turned_hn", i][:].rearrange("p g u b -> p g b u"),
            )
            st["hn_words", i] = hn_words

        def quantise_hn(i):
            codes = work.tile([P, 2 * P], U32, align_bytes=64, tag="hn_codes", name="hn_codes")
            plane = work.tile([P, 2 * P], U8, align_bytes=64, tag="hn_plane", name="hn_plane")
            nc.vector.quantize_mx(out=codes[:].bitcast(FP8X4), scales=plane[:], in_=st["hn_words", i][:])
            st["hn_codes", i], st["hn_plane", i] = codes, plane

        def multiply_w2(i):
            acc = psum.tile([P, D], F32, tag="out", bufs=1, name="acc2")
            for g in range(2):
                part = slice(P * g, P * g + P)
                nc.tensor.matmul_mx(
                    out=acc[:],
                    lhsT=st["hn_codes", i][:, part].bitcast(FP8X4),
                    lhsT_scale=st["hn_plane", i][:, part],
                    rhs=w2_codes[:, g, :].bitcast(FP8X4),
                    rhs_scale=w2_planes[:, g, :],
                    start=(g == 0),
                    stop=(g == 1),
                )
            st["acc2", i] = acc

        def add_b2(i):
            prediction = work.tile([P, D], F32, tag="prediction", name="prediction")
            nc.vector.tensor_tensor(out=prediction[:], in0=st["acc2", i][:], in1=b2_all[:], op=ALU.add)
            st["prediction", i] = prediction

        def fill_slots(i, slots, on_vector=()):
            if slots[0] == 0:
                st["slots", i] = outp.tile([P, T, D], F32, tag="slots", name="slots")
            for j in slots:
                mask = valid[:, i, j : j + 1]
                dst = st["slots", i][:, j, :]
                if j in on_vector:
                    nc.vector.tensor_scalar_mul(dst, st["prediction", i][:], mask)
                else:
                    nc.scalar.activation(out=dst, in_=st["prediction", i][:], func=ACT.Copy, scale=mask)

        def store_slots(i, slots):
            part = slice(slots[0], slots[0] + len(slots))
            nc.sync.dma_start(out=out[P * i : P * i + P, part, :], in_=st["slots", i][:, part, :])

        nc.vector.tensor_reduce(out=count[:], in_=cmask[:], axis=X, op=ALU.add)
        nc.vector.tensor_scalar_max(count_or_1[:], count[:], 1.0)
        nc.vector.reciprocal(reciprocal[:], count_or_1[:])
        nc.vector.scalar_tensor_tensor(
            out=factor[:], in0=count[:], scalar=0.0, in1=reciprocal[:], op0=ALU.is_gt, op1=ALU.mult
        )
        b1_all = spread_hidden(b1_cols, "b1_all")
        interleave_w1(0)
        interleave_w1(1)
        spread_factor(0)
        pool(0, 0)
        spread_factor(1)
        pool(0, 1)
        pool(0, 2)
        pool(0, 3)
        quantise_w1(0)
        quantise_w1(1)
        load_rows(4)
        scale_mean(0)

        target_n = keep.tile([P, 8], F32)
        nc.vector.tensor_reduce(out=target_n[:], in_=tmask[:], axis=X, op=ALU.add)
        nc.vector.tensor_copy(out=sel1[:], in_=sel1_f32[:])
        quantise_mean(0)
        multiply_w1(0)
        picked = keep.tile([P, 16, 8], BF16)
        nc.vector.tensor_tensor(
            out=picked[:],
            in0=target_n[:].unsqueeze(1).to_broadcast([P, 16, 8]),
            in1=mod16[:].unsqueeze(2).to_broadcast([P, 16, 8]),
            op=ALU.mult,
        )
        widen_w2(0)
        n_of_row = keep.tile([P, NT], F32)
        valid = keep.tile([P, NT, T], F32)

        for s in range(NT):
            nxt = s + 1
            if 0 < s < NT - 4:
                load_rows(s + 4)
            if s >= 2:
                interleave_hn(s - 2)
            if s >= 3:
                fill_slots(s - 3, HIGH)
                store_slots(s - 3, LOW + HIGH if s - 3 < FIRST_HALF_STORED else HIGH)
            if nxt < NT:
                if s == 0:
                    pool(nxt, 0)
                    pool(nxt, 1)
                pool(nxt, 2)
                if s != 2:
                    pool(nxt, 3)
            if s >= 1:
                half_statistics(s - 1, 0)
                half_statistics(s - 1, 1)
            bias_and_gelu(s, 0)
            if s >= 1:
                statistics(s - 1)
            if s == 2:
                quantise_w2(1)
            if s >= 2:
                quantise_hn(s - 2)
                multiply_w2(s - 2)
            if s == 2:
                pool(nxt, 3)
            if 1 <= s < NT - 2:
                pool(s + 2, 0)
                pool(s + 2, 1)
            bias_and_gelu(s, 1)

            if s == 0:
                interleave_w2(0)
                gamma_all = spread_hidden(gamma_cols, "gamma_all")
                beta_all = spread_hidden(beta_cols, "beta_all")
                widen_w2(1)
                n_psum = psum.tile([P, NT], F32, tag="out", bufs=1, name="n_psum")
                nc.tensor.matmul(
                    out=n_psum[:], lhsT=picked[:].rearrange("p q i -> p (q i)"), rhs=sel1[:], start=True, stop=True
                )
            if s == 1:
                nc.vector.tensor_copy(out=n_of_row[:], in_=n_psum[:])
                interleave_w2(1)
                b2_all = keep.tile([P, D], BF16)
                nc.scalar.copy(
                    out=b2_all[:].rearrange("p (n i) -> p n i", i=4),
                    in_=turn_vector(b2_cols, 4)[:].rearrange("p i n -> p n i"),
                )
                quantise_w2(0)

            if s >= 1:
                centre(s - 1)
            if s >= 2:
                add_b2(s - 2)
                fill_slots(s - 2, LOW)
                if s - 2 >= FIRST_HALF_STORED:
                    store_slots(s - 2, LOW)
            if nxt < NT:
                scale_mean(nxt)
            if s == 1:
                nc.vector.tensor_tensor(
                    out=valid[:],
                    in0=slot_index[:].unsqueeze(1).to_broadcast([P, NT, T]),
                    in1=n_of_row[:].unsqueeze(2).to_broadcast([P, NT, T]),
                    op=ALU.is_lt,
                )
            if s == 0:
                pool(s + 2, 0)
            if s >= 1:
                normalise(s - 1)
                transpose_hn(s - 1)
            if nxt < NT:
                quantise_mean(nxt)
                multiply_w1(nxt)
            if s == 0:
                pool(s + 2, 1)

        interleave_hn(LAST - 1)
        fill_slots(LAST - 2, HIGH)
        store_slots(LAST - 2, HIGH)
        half_statistics(LAST, 0)
        half_statistics(LAST, 1)
        statistics(LAST)
        centre(LAST)
        quantise_hn(LAST - 1)
        multiply_w2(LAST - 1)
        normalise(LAST)
        transpose_hn(LAST)
        add_b2(LAST - 1)
        interleave_hn(LAST)
        fill_slots(LAST - 1, LOW, on_vector=(1, 2, 3))
        store_slots(LAST - 1, LOW)
        quantise_hn(LAST)
        multiply_w2(LAST)
        fill_slots(LAST - 1, HIGH, on_vector=(6, 7))
        store_slots(LAST - 1, HIGH)
        add_b2(LAST)
        for j in range(0, T, 2):
            pair = (j, j + 1)
            fill_slots(LAST, pair, on_vector=pair if j == T - 2 else (j + 1,))
            store_slots(LAST, pair)
